import numpy as np
import ml_dtypes


def mxq(x, axis, fmt="e4m3"):
    dtype, down = {"e4m3": (ml_dtypes.float8_e4m3fn, 7), "e5m2": (ml_dtypes.float8_e5m2, 14)}[fmt]
    v = np.moveaxis(np.asarray(x, np.float32).astype(ml_dtypes.bfloat16).astype(np.float64), axis, -1)
    blocks = v.reshape(v.shape[:-1] + (-1, 32))
    amax = np.abs(blocks).max(-1, keepdims=True)
    byte = np.maximum(np.where(amax > 0, np.frexp(amax)[1] - 1 + 127, 0) - down, 1)
    scale = np.exp2(byte - 127.0)
    codes = (blocks / scale).astype(np.float32).astype(dtype).astype(np.float64)
    return np.moveaxis((codes * scale).reshape(v.shape), -1, axis)


WIDE = False


def mx_kscale(k):
    if not WIDE:
        return np.ones(k)
    levels = np.array([10, -10, 5, -5, 0])
    if k % 512:
        return np.exp2(np.random.permutation(np.resize(levels, k // 32))).repeat(32)
    a = np.empty((k // 512, 16))
    for p in range(k // 512):
        a[p, :8] = np.random.permutation(np.resize(levels, 8))
        for g in range(8):
            far = levels[np.abs(levels - a[p, g]) >= 10]
            a[p, g + 8] = far[np.random.randint(len(far))]
    return np.exp2(a.ravel()).repeat(32)


BF16 = ml_dtypes.bfloat16


def bf(x):
    return np.asarray(x, np.float32).astype(BF16)


def f64(x):
    return np.asarray(x).astype(np.float64)


B, S, DIM, N_HEADS, HEAD_DIM, F = 2, 512, 1024, 8, 128, 4096
QD = N_HEADS * HEAD_DIM
THETA = 10000.0
EPS = 1e-6


def rms_norm(x, w):
    return x * (1.0 / np.sqrt(np.mean(x * x, axis=-1, keepdims=True) + EPS)) * w


def rope_tables():
    inv = 1.0 / THETA ** (np.arange(0, HEAD_DIM, 2) / HEAD_DIM)
    freqs = np.outer(np.arange(S), inv)
    return np.cos(freqs), np.sin(freqs)


def rot(u, cos, sin):
    c = cos[None, :, None, :]
    s = sin[None, :, None, :]
    ur, ui = u[..., 0::2], u[..., 1::2]
    yr = ur * c - ui * s
    yi = ur * s + ui * c
    return np.stack([yr, yi], axis=-1).reshape(u.shape)


def setup_inputs():
    s = mx_kscale(DIM)
    sc = 1.0 / np.sqrt(DIM)
    quiet = np.where(np.random.random((B, S, 1)) < 0.125, 1e-3, 1.0)
    return {"x": bf(np.random.standard_normal((B, S, DIM)) * quiet),
            "attn_norm_w": bf((1.0 + 0.1 * np.random.standard_normal(DIM)) * s),
            "wq": bf(np.random.standard_normal((DIM, QD)) * sc / s[:, None]),
            "wk": bf(np.random.standard_normal((DIM, QD)) * sc / s[:, None]),
            "wv": bf(np.random.standard_normal((DIM, QD)) * sc / s[:, None])}


def reference(x, attn_norm_w, wq, wk, wv):
    h = rms_norm(f64(x), f64(attn_norm_w))
    hq = mxq(h, 2, "e4m3")
    q = (hq @ mxq(f64(wq), 0, "e4m3")).reshape(B, S, N_HEADS, HEAD_DIM)
    k = (hq @ mxq(f64(wk), 0, "e4m3")).reshape(B, S, N_HEADS, HEAD_DIM)
    v = (hq @ mxq(f64(wv), 0, "e4m3")).reshape(B, S, N_HEADS, HEAD_DIM)
    cos, sin = rope_tables()
    q = rot(q, cos, sin)
    k = rot(k, cos, sin)
    return q.transpose(0, 2, 1, 3), k.transpose(0, 2, 1, 3), v.transpose(0, 2, 1, 3)

@@ -1,0 +1,280 @@
+import math
+from contextlib import ExitStack
+
+import concourse.mybir as mybir
+from concourse.masks import make_identity
+
+FP8X4 = mybir.dt.float8_e4m3fn_x4
+BF16 = mybir.dt.bfloat16
+F32 = mybir.dt.float32
+I32 = mybir.dt.int32
+U32 = mybir.dt.uint32
+U8 = mybir.dt.uint8
+ALU = mybir.AluOpType
+ACT = mybir.ActivationFunctionType
+
+P = 128
+BATCH = 2
+SEQ = 512
+DIM = 1024
+HEADS = 8
+HEAD_DIM = 128
+PAIRS = HEAD_DIM // 2
+QD = HEADS * HEAD_DIM
+THETA = 10000.0
+EPS = 1e-6
+
+PACK = 4
+K_PASS = P * PACK
+PASSES = DIM // K_PASS
+SUB = SEQ // P
+N_TILE = 512
+N_HEADS = N_TILE // HEAD_DIM
+N_CHUNKS = QD // N_TILE
+K_PAIRS = PACK // 2
+
+ROUND_MAGIC = 12582912.0
+
+FLOPS = 2 * BATCH * SEQ * DIM * 3 * QD
+
+
+def tile_flexattentionblock_pa_kernel(tc, x, attn_norm_w, wq, wk, wv, out_0, out_1, out_2):
+    nc = tc.nc
+    weights = (wq, wk, wv)
+    outs = (out_0, out_1, out_2)
+    Q, K, V = 0, 1, 2
+
+    with ExitStack() as ctx:
+        const = ctx.enter_context(tc.tile_pool(name="const", bufs=1))
+        resident = ctx.enter_context(tc.tile_pool(name="resident", bufs=1))
+        squares_pool = ctx.enter_context(tc.tile_pool(name="squares", bufs=2))
+        h_pool = ctx.enter_context(tc.tile_pool(name="h", bufs=3))
+        w_grouped_pool = ctx.enter_context(tc.tile_pool(name="w_grouped", bufs=4))
+        rot_pool = ctx.enter_context(tc.tile_pool(name="rot", bufs=4))
+        y_pool = ctx.enter_context(tc.tile_pool(name="y", bufs=5))
+        psum_t = ctx.enter_context(tc.psum_pool(name="psum_t", bufs=2))
+        psum = ctx.enter_context(tc.psum_pool(name="psum", bufs=6))
+
+        gain_row = const.tile([P, DIM], BF16)
+        nc.vector.memset(gain_row[:], 0.0)
+        nc.sync.dma_start(out=gain_row[0:1, :], in_=attn_norm_w.rearrange("(o k) -> o k", o=1))
+
+        x_sb = [resident.tile([P, SUB, DIM], BF16, name="x_sb%d" % b) for b in range(BATCH)]
+        w_raw = [
+            [resident.tile([P, PACK, QD], BF16, name="w_raw%d_%d" % (m, g)) for g in range(PASSES)]
+            for m in range(3)
+        ]
+
+        def load_x(b):
+            nc.sync.dma_start(out=x_sb[b][:], in_=x[b, :, :].rearrange("(p s) k -> p s k", s=SUB))
+
+        def load_weight(m):
+            by_pass = weights[m].rearrange("(g p t) n -> g p t n", t=PACK, p=P)
+            for g in range(PASSES):
+                nc.sync.dma_start(out=w_raw[m][g][:], in_=by_pass[g, :, :, :])
+
+        load_x(0)
+        load_weight(Q)
+        load_x(1)
+        load_weight(K)
+        load_weight(V)
+
+        ident = const.tile([P, P], F32)
+        make_identity(nc, ident[:])
+        ones = const.tile([P, P], BF16)
+        nc.vector.memset(ones[:], 1.0)
+        neg_half = const.tile([P, 1], F32)
+        nc.vector.memset(neg_half[:], -0.5)
+
+        gain = const.tile([P, DIM], BF16)
+        for half in range(DIM // N_TILE):
+            cols = slice(half * N_TILE, (half + 1) * N_TILE)
+            spread = psum.tile([P, N_TILE], F32, tag="acc")
+            nc.tensor.matmul(out=spread[:], lhsT=ones[:], rhs=gain_row[:, cols], start=True, stop=True)
+            nc.scalar.copy(out=gain[:, cols], in_=spread[:])
+
+        freq = const.tile([P, PAIRS], F32)
+        nc.vector.memset(freq[:, 0:1], 1.0)
+        width = 1
+        while width < PAIRS:
+            nc.vector.tensor_scalar_mul(
+                out=freq[:, width : 2 * width], in0=freq[:, 0:width], scalar1=THETA ** (-2.0 * width / HEAD_DIM)
+            )
+            width *= 2
+
+        pos_int = const.tile([P, SUB], I32)
+        nc.gpsimd.iota(pos_int[:], pattern=[[1, SUB]], base=0, channel_multiplier=SUB)
+        pos = const.tile([P, SUB], F32)
+        nc.vector.tensor_copy(out=pos[:], in_=pos_int[:])
+
+        table_shape = [P, SUB, PAIRS]
+        turns = const.tile(table_shape, F32)
+        nc.vector.scalar_tensor_tensor(
+            out=turns[:],
+            in0=freq[:].unsqueeze(1).to_broadcast(table_shape),
+            scalar=1.0 / (2.0 * math.pi),
+            in1=pos[:].unsqueeze(2).to_broadcast(table_shape),
+            op0=ALU.mult,
+            op1=ALU.mult,
+        )
+        EVEN, ODD = 0, 1
+        angle = const.tile([P, SUB, 2, PAIRS, 2], F32)
+        whole = const.tile(table_shape, F32)
+        nc.vector.tensor_scalar(
+            out=whole[:], in0=turns[:], scalar1=ROUND_MAGIC, scalar2=ROUND_MAGIC, op0=ALU.add, op1=ALU.subtract
+        )
+        nc.vector.tensor_tensor(out=angle[:, :, EVEN, :, 1], in0=turns[:], in1=whole[:], op=ALU.subtract)
+        nc.vector.tensor_tensor(out=angle[:, :, ODD, :, 0], in0=whole[:], in1=turns[:], op=ALU.subtract)
+        shifted = const.tile(table_shape, F32)
+        nc.vector.tensor_scalar_add(out=shifted[:], in0=angle[:, :, EVEN, :, 1], scalar1=0.25)
+        whole_shifted = const.tile(table_shape, F32)
+        nc.vector.tensor_scalar(
+            out=whole_shifted[:], in0=shifted[:], scalar1=ROUND_MAGIC, scalar2=ROUND_MAGIC, op0=ALU.add, op1=ALU.subtract
+        )
+        nc.vector.tensor_tensor(out=angle[:, :, EVEN, :, 0], in0=shifted[:], in1=whole_shifted[:], op=ALU.subtract)
+        nc.vector.tensor_tensor(out=angle[:, :, ODD, :, 1], in0=shifted[:], in1=whole_shifted[:], op=ALU.subtract)
+        factors = const.tile([P, SUB, 2, PAIRS, 2], F32)
+        nc.scalar.activation(out=factors[:], in_=angle[:], func=ACT.Sin, scale=2.0 * math.pi)
+
+        h_codes = resident.tile([P, BATCH * SUB * PASSES * P], U32, align_bytes=64)
+        h_scales = resident.tile([P, BATCH * SUB * PASSES * P], U8, align_bytes=64)
+        mean_sq = const.tile([P, BATCH * SUB], F32)
+        mean_eps = const.tile([P, BATCH * SUB], F32)
+        rstd = const.tile([P, BATCH * SUB], F32)
+
+        def quantise_token_tile(b, s):
+            i = b * SUB + s
+            one = slice(i, i + 1)
+            x_tile = x_sb[b][:, s, :]
+            squares = squares_pool.tile([P, DIM], BF16)
+            nc.scalar.activation(
+                out=squares[:], in_=x_tile, func=ACT.Square, scale=1.0 / math.sqrt(DIM), accum_out=mean_sq[:, one]
+            )
+            nc.gpsimd.tensor_scalar(out=mean_eps[:, one], in0=mean_sq[:, one], scalar1=EPS, scalar2=None, op0=ALU.add)
+            nc.gpsimd.tensor_tensor(out=rstd[:, one], in0=mean_eps[:, one], in1=neg_half[:], op=ALU.pow)
+            h = h_pool.tile([P, DIM], BF16)
+            nc.vector.scalar_tensor_tensor(
+                out=h[:], in0=x_tile, scalar=rstd[:, one], in1=gain[:], op0=ALU.mult, op1=ALU.mult
+            )
+            words = h[:].bitcast(F32)
+            h_t = psum_t.tile([P, PASSES, K_PAIRS, P], F32)
+            for g in range(PASSES):
+                for u in range(K_PAIRS):
+                    nc.tensor.transpose(
+                        h_t[:, g, u, :], words[:, K_PAIRS * P * g + u : K_PAIRS * P * (g + 1) : K_PAIRS], ident[:]
+                    )
+            h_grouped = h_pool.tile([P, PASSES * P * PACK], BF16, align_bytes=64)
+            nc.scalar.copy(
+                out=h_grouped[:].bitcast(F32).rearrange("p (g r u) -> p g r u", g=PASSES, u=K_PAIRS),
+                in_=h_t[:].rearrange("p g u r -> p g r u"),
+            )
+            cols = slice(i * PASSES * P, (i + 1) * PASSES * P)
+            nc.vector.quantize_mx(
+                out=h_codes[:, cols].bitcast(FP8X4),
+                scales=h_scales[:, cols],
+                in_=h_grouped[:],
+            )
+
+        w_codes = [resident.tile([P, PASSES, QD], U32, name="w_codes%d" % m, align_bytes=64) for m in range(3)]
+        w_scales = [resident.tile([P, PASSES, QD], U8, name="w_scales%d" % m, align_bytes=64) for m in range(3)]
+
+        def quantise_weight_chunk(m, c, copy):
+            cols = slice(c * N_TILE, (c + 1) * N_TILE)
+            grouped = []
+            for g in range(PASSES):
+                w_grouped = w_grouped_pool.tile([P, N_TILE, PACK], BF16, align_bytes=64)
+                copy(
+                    out=w_grouped[:].rearrange("p (a i) t -> p a t i", i=4),
+                    in_=w_raw[m][g][:, :, cols].rearrange("p t (a i) -> p a t i", i=4),
+                )
+                grouped.append(w_grouped)
+            for g in range(PASSES):
+                nc.vector.quantize_mx(
+                    out=w_codes[m][:, g, cols].bitcast(FP8X4),
+                    scales=w_scales[m][:, g, cols],
+                    in_=grouped[g][:].rearrange("p n t -> p (n t)"),
+                )
+
+        def project(m, b, s, c):
+            i = b * SUB + s
+            cols = slice(c * N_TILE, (c + 1) * N_TILE)
+            acc = psum.tile([P, N_TILE], F32, tag="acc")
+            for g in range(PASSES):
+                tokens = slice((i * PASSES + g) * P, (i * PASSES + g + 1) * P)
+                nc.tensor.matmul_mx(
+                    out=acc[:],
+                    lhsT=h_codes[:, tokens].bitcast(FP8X4),
+                    lhsT_scale=h_scales[:, tokens],
+                    rhs=w_codes[m][:, g, cols].bitcast(FP8X4),
+                    rhs_scale=w_scales[m][:, g, cols],
+                    start=(g == 0),
+                    stop=(g == PASSES - 1),
+                )
+            return acc
+
+        rot_shape = [P, N_HEADS, PAIRS, 2]
+
+        def rotate(acc, s, y):
+            by_parity = acc[:].rearrange("p (h j e) -> p e h j", j=PAIRS, e=2)
+            share = []
+            for parity in (EVEN, ODD):
+                product = rot_pool.tile(rot_shape, F32, name="share%d" % parity)
+                nc.vector.tensor_tensor(
+                    out=product[:],
+                    in0=by_parity[:, parity, :, :].unsqueeze(3).to_broadcast(rot_shape),
+                    in1=factors[:, s, parity, :, :].unsqueeze(1).to_broadcast(rot_shape),
+                    op=ALU.mult,
+                )
+                share.append(product)
+            nc.gpsimd.tensor_tensor(
+                out=y,
+                in0=share[EVEN][:].rearrange("p h j r -> p h (j r)"),
+                in1=share[ODD][:].rearrange("p h j r -> p h (j r)"),
+                op=ALU.add,
+            )
+
+        def new_result():
+            y_tile = y_pool.tile([P, N_HEADS, SUB, HEAD_DIM], F32)
+            return y_tile
+
+        def store(m, b, c, y_tile):
+            heads = slice(c * N_HEADS, (c + 1) * N_HEADS)
+            nc.sync.dma_start(
+                out=outs[m][b, heads, :, :].rearrange("h (p s) d -> p h (s d)", s=SUB),
+                in_=y_tile[:].rearrange("p h s d -> p h (s d)"),
+            )
+
+        def rotated_unit(m, b, s, c, y_tile):
+            rotate(project(m, b, s, c), s, y_tile[:, :, s, :])
+
+        def plain_unit(m, b, s, c, y_tile):
+            acc = project(m, b, s, c)
+            nc.scalar.copy(out=y_tile[:, :, s, :], in_=acc[:].rearrange("p (h d) -> p h d", d=HEAD_DIM))
+
+        for s in range(SUB):
+            quantise_token_tile(0, s)
+        for c in range(N_CHUNKS):
+            quantise_weight_chunk(Q, c, nc.vector.tensor_copy)
+        for c in range(N_CHUNKS):
+            y_q = new_result()
+            for s in range(SUB):
+                rotated_unit(Q, 0, s, c, y_q)
+            store(Q, 0, c, y_q)
+        for s in range(SUB):
+            quantise_token_tile(1, s)
+        for c in range(N_CHUNKS):
+            y_q = new_result()
+            for s in range(SUB):
+                rotated_unit(Q, 1, s, c, y_q)
+            store(Q, 1, c, y_q)
+        for c in range(N_CHUNKS):
+            quantise_weight_chunk(K, c, nc.scalar.copy)
+            quantise_weight_chunk(V, c, nc.scalar.copy)
+            for b in range(BATCH):
+                y_k = new_result()
+                y_v = new_result()
+                for s in range(SUB):
+                    rotated_unit(K, b, s, c, y_k)
+                    plain_unit(V, b, s, c, y_v)
+                store(V, b, c, y_v)
+                store(K, b, c, y_k)

@@ -33,6 +33,8 @@ N_HEADS = N_TILE // HEAD_DIM
 N_CHUNKS = QD // N_TILE
 K_PAIRS = PACK // 2
 
+LOOKAHEAD = 2
+
 ROUND_MAGIC = 12582912.0
 
 FLOPS = 2 * BATCH * SEQ * DIM * 3 * QD
@@ -48,233 +50,327 @@ def tile_flexattentionblock_pa_kernel(tc, x, attn_norm_w, wq, wk, wv, out_0, out
         const = ctx.enter_context(tc.tile_pool(name="const", bufs=1))
         resident = ctx.enter_context(tc.tile_pool(name="resident", bufs=1))
         squares_pool = ctx.enter_context(tc.tile_pool(name="squares", bufs=2))
-        h_pool = ctx.enter_context(tc.tile_pool(name="h", bufs=3))
-        w_grouped_pool = ctx.enter_context(tc.tile_pool(name="w_grouped", bufs=4))
+        h_pool = ctx.enter_context(tc.tile_pool(name="h", bufs=4))
+        w_grouped_pool = ctx.enter_context(tc.tile_pool(name="w_grouped", bufs=3))
         rot_pool = ctx.enter_context(tc.tile_pool(name="rot", bufs=4))
         y_pool = ctx.enter_context(tc.tile_pool(name="y", bufs=5))
-        psum_t = ctx.enter_context(tc.psum_pool(name="psum_t", bufs=2))
-        psum = ctx.enter_context(tc.psum_pool(name="psum", bufs=6))
+        psum_gain = ctx.enter_context(tc.psum_pool(name="psum_gain", bufs=1))
+        psum_aux = ctx.enter_context(tc.psum_pool(name="psum_aux", bufs=2))
+        psum = ctx.enter_context(tc.psum_pool(name="psum", bufs=4))
+        ctx.enter_context(tc.manual_schedule())
+
+        sin_probe = const.tile([P, 1], F32)
+        nc.vector.memset(sin_probe[:], 0.0)
+        nc.scalar.activation(out=sin_probe[:], in_=sin_probe[:], func=ACT.Sin)
 
         gain_row = const.tile([P, DIM], BF16)
-        nc.vector.memset(gain_row[:], 0.0)
-        nc.sync.dma_start(out=gain_row[0:1, :], in_=attn_norm_w.rearrange("(o k) -> o k", o=1))
+        nc.gpsimd.memset(gain_row[:].bitcast(I32), 0)
 
         x_sb = [resident.tile([P, SUB, DIM], BF16, name="x_sb%d" % b) for b in range(BATCH)]
+        wq_raw = [resident.tile([P, PASSES, PACK, N_TILE], BF16, name="wq_raw%d" % c) for c in range(N_CHUNKS)]
         w_raw = [
             [resident.tile([P, PACK, QD], BF16, name="w_raw%d_%d" % (m, g)) for g in range(PASSES)]
-            for m in range(3)
+            for m in (K, V)
         ]
+        by_pass = [w.rearrange("(g p t) n -> g p t n", t=PACK, p=P) for w in weights]
 
-        def load_x(b):
-            nc.sync.dma_start(out=x_sb[b][:], in_=x[b, :, :].rearrange("(p s) k -> p s k", s=SUB))
+        def load_x(b, s):
+            nc.sync.dma_start(out=x_sb[b][:, s, :], in_=x[b, :, :].rearrange("(p s) k -> p s k", s=SUB)[:, s, :])
+
+        def load_wq(c):
+            for g in range(PASSES):
+                nc.sync.dma_start(
+                    out=wq_raw[c][:, g, :, :], in_=by_pass[Q][g, :, :, c * N_TILE : (c + 1) * N_TILE]
+                )
 
         def load_weight(m):
-            by_pass = weights[m].rearrange("(g p t) n -> g p t n", t=PACK, p=P)
             for g in range(PASSES):
-                nc.sync.dma_start(out=w_raw[m][g][:], in_=by_pass[g, :, :, :])
+                nc.sync.dma_start(out=w_raw[m - K][g][:], in_=by_pass[m][g, :, :, :])
 
-        load_x(0)
-        load_weight(Q)
-        load_x(1)
+        load_x(0, 0)
+        nc.sync.dma_start(out=gain_row[0:1, :], in_=attn_norm_w.rearrange("(o k) -> o k", o=1))
+        for s in range(1, SUB):
+            load_x(0, s)
+        load_wq(0)
+        load_wq(1)
+        nc.sync.dma_start(out=x_sb[1][:], in_=x[1, :, :].rearrange("(p s) k -> p s k", s=SUB))
         load_weight(K)
         load_weight(V)
 
         ident = const.tile([P, P], F32)
         make_identity(nc, ident[:])
         ones = const.tile([P, P], BF16)
-        nc.vector.memset(ones[:], 1.0)
+        nc.gpsimd.memset(ones[:], 1.0)
         neg_half = const.tile([P, 1], F32)
-        nc.vector.memset(neg_half[:], -0.5)
+        nc.gpsimd.memset(neg_half[:], -0.5)
 
-        gain = const.tile([P, DIM], BF16)
+        gain = []
         for half in range(DIM // N_TILE):
-            cols = slice(half * N_TILE, (half + 1) * N_TILE)
-            spread = psum.tile([P, N_TILE], F32, tag="acc")
-            nc.tensor.matmul(out=spread[:], lhsT=ones[:], rhs=gain_row[:, cols], start=True, stop=True)
-            nc.scalar.copy(out=gain[:, cols], in_=spread[:])
+            spread = psum_gain.tile([P, N_TILE], F32, name="gain%d" % half)
+            nc.tensor.matmul(
+                out=spread[:], lhsT=ones[:], rhs=gain_row[:, half * N_TILE : (half + 1) * N_TILE], start=True, stop=True
+            )
+            gain.append(spread)
 
         freq = const.tile([P, PAIRS], F32)
-        nc.vector.memset(freq[:, 0:1], 1.0)
-        width = 1
-        while width < PAIRS:
-            nc.vector.tensor_scalar_mul(
-                out=freq[:, width : 2 * width], in0=freq[:, 0:width], scalar1=THETA ** (-2.0 * width / HEAD_DIM)
-            )
-            width *= 2
-
         pos_int = const.tile([P, SUB], I32)
-        nc.gpsimd.iota(pos_int[:], pattern=[[1, SUB]], base=0, channel_multiplier=SUB)
         pos = const.tile([P, SUB], F32)
-        nc.vector.tensor_copy(out=pos[:], in_=pos_int[:])
-
         table_shape = [P, SUB, PAIRS]
+        pair_shape = [P, SUB, PAIRS, 2]
         turns = const.tile(table_shape, F32)
-        nc.vector.scalar_tensor_tensor(
-            out=turns[:],
-            in0=freq[:].unsqueeze(1).to_broadcast(table_shape),
-            scalar=1.0 / (2.0 * math.pi),
-            in1=pos[:].unsqueeze(2).to_broadcast(table_shape),
-            op0=ALU.mult,
-            op1=ALU.mult,
-        )
-        EVEN, ODD = 0, 1
-        angle = const.tile([P, SUB, 2, PAIRS, 2], F32)
         whole = const.tile(table_shape, F32)
-        nc.vector.tensor_scalar(
-            out=whole[:], in0=turns[:], scalar1=ROUND_MAGIC, scalar2=ROUND_MAGIC, op0=ALU.add, op1=ALU.subtract
-        )
-        nc.vector.tensor_tensor(out=angle[:, :, EVEN, :, 1], in0=turns[:], in1=whole[:], op=ALU.subtract)
-        nc.vector.tensor_tensor(out=angle[:, :, ODD, :, 0], in0=whole[:], in1=turns[:], op=ALU.subtract)
         shifted = const.tile(table_shape, F32)
-        nc.vector.tensor_scalar_add(out=shifted[:], in0=angle[:, :, EVEN, :, 1], scalar1=0.25)
         whole_shifted = const.tile(table_shape, F32)
-        nc.vector.tensor_scalar(
-            out=whole_shifted[:], in0=shifted[:], scalar1=ROUND_MAGIC, scalar2=ROUND_MAGIC, op0=ALU.add, op1=ALU.subtract
-        )
-        nc.vector.tensor_tensor(out=angle[:, :, EVEN, :, 0], in0=shifted[:], in1=whole_shifted[:], op=ALU.subtract)
-        nc.vector.tensor_tensor(out=angle[:, :, ODD, :, 1], in0=shifted[:], in1=whole_shifted[:], op=ALU.subtract)
-        factors = const.tile([P, SUB, 2, PAIRS, 2], F32)
-        nc.scalar.activation(out=factors[:], in_=angle[:], func=ACT.Sin, scale=2.0 * math.pi)
+        cos_turns = const.tile(table_shape, F32)
+        sin_turns = const.tile(pair_shape, F32)
+        cos_table = const.tile(pair_shape, F32)
+        sin_table = const.tile(pair_shape, F32)
+
+        def make_turns():
+            nc.gpsimd.iota(pos_int[:], pattern=[[1, SUB]], base=0, channel_multiplier=SUB)
+            nc.vector.memset(freq[:, 0:1], 1.0)
+            width = 1
+            while width < PAIRS:
+                nc.vector.tensor_scalar_mul(
+                    out=freq[:, width : 2 * width], in0=freq[:, 0:width], scalar1=THETA ** (-2.0 * width / HEAD_DIM)
+                )
+                width *= 2
+            nc.vector.tensor_copy(out=pos[:], in_=pos_int[:])
+            nc.vector.scalar_tensor_tensor(
+                out=turns[:],
+                in0=freq[:].unsqueeze(1).to_broadcast(table_shape),
+                scalar=1.0 / (2.0 * math.pi),
+                in1=pos[:].unsqueeze(2).to_broadcast(table_shape),
+                op0=ALU.mult,
+                op1=ALU.mult,
+            )
+
+        def round_off(out, in_):
+            nc.vector.tensor_scalar(
+                out=out, in0=in_, scalar1=ROUND_MAGIC, scalar2=ROUND_MAGIC, op0=ALU.add, op1=ALU.subtract
+            )
+
+        def make_sin_turns():
+            nc.vector.tensor_tensor(out=sin_turns[:, :, :, 1], in0=turns[:], in1=whole[:], op=ALU.subtract)
+            nc.vector.tensor_tensor(out=sin_turns[:, :, :, 0], in0=whole[:], in1=turns[:], op=ALU.subtract)
+
+        def shift_turns():
+            nc.vector.tensor_scalar_add(out=shifted[:], in0=turns[:], scalar1=0.25)
+
+        def make_cos_turns():
+            nc.vector.tensor_tensor(out=cos_turns[:], in0=shifted[:], in1=whole_shifted[:], op=ALU.subtract)
+
+        def make_tables():
+            nc.scalar.activation(out=sin_table[:], in_=sin_turns[:], func=ACT.Sin, scale=2.0 * math.pi)
+            nc.scalar.activation(
+                out=cos_table[:], in_=cos_turns[:].unsqueeze(3).to_broadcast(pair_shape), func=ACT.Sin, scale=2.0 * math.pi
+            )
 
         h_codes = resident.tile([P, BATCH * SUB * PASSES * P], U32, align_bytes=64)
         h_scales = resident.tile([P, BATCH * SUB * PASSES * P], U8, align_bytes=64)
         mean_sq = const.tile([P, BATCH * SUB], F32)
         mean_eps = const.tile([P, BATCH * SUB], F32)
         rstd = const.tile([P, BATCH * SUB], F32)
+        h_planes = {}
+        h_words = {}
 
-        def quantise_token_tile(b, s):
-            i = b * SUB + s
-            one = slice(i, i + 1)
-            x_tile = x_sb[b][:, s, :]
+        def square(b, s):
+            one = slice(b * SUB + s, b * SUB + s + 1)
             squares = squares_pool.tile([P, DIM], BF16)
             nc.scalar.activation(
-                out=squares[:], in_=x_tile, func=ACT.Square, scale=1.0 / math.sqrt(DIM), accum_out=mean_sq[:, one]
+                out=squares[:], in_=x_sb[b][:, s, :], func=ACT.Square, scale=1.0 / math.sqrt(DIM), accum_out=mean_sq[:, one]
             )
             nc.gpsimd.tensor_scalar(out=mean_eps[:, one], in0=mean_sq[:, one], scalar1=EPS, scalar2=None, op0=ALU.add)
             nc.gpsimd.tensor_tensor(out=rstd[:, one], in0=mean_eps[:, one], in1=neg_half[:], op=ALU.pow)
+
+        def normalise(b, s):
+            one = slice(b * SUB + s, b * SUB + s + 1)
             h = h_pool.tile([P, DIM], BF16)
-            nc.vector.scalar_tensor_tensor(
-                out=h[:], in0=x_tile, scalar=rstd[:, one], in1=gain[:], op0=ALU.mult, op1=ALU.mult
-            )
+            for half in range(DIM // N_TILE):
+                cols = slice(half * N_TILE, (half + 1) * N_TILE)
+                nc.vector.scalar_tensor_tensor(
+                    out=h[:, cols],
+                    in0=x_sb[b][:, s, cols],
+                    scalar=rstd[:, one],
+                    in1=gain[half][:],
+                    op0=ALU.mult,
+                    op1=ALU.mult,
+                )
             words = h[:].bitcast(F32)
-            h_t = psum_t.tile([P, PASSES, K_PAIRS, P], F32)
+            h_t = psum_aux.tile([P, PASSES, K_PAIRS, P], F32, tag="aux")
             for g in range(PASSES):
                 for u in range(K_PAIRS):
                     nc.tensor.transpose(
                         h_t[:, g, u, :], words[:, K_PAIRS * P * g + u : K_PAIRS * P * (g + 1) : K_PAIRS], ident[:]
                     )
+            h_planes[b, s] = h_t
+
+        def group_h(b, s):
             h_grouped = h_pool.tile([P, PASSES * P * PACK], BF16, align_bytes=64)
             nc.scalar.copy(
                 out=h_grouped[:].bitcast(F32).rearrange("p (g r u) -> p g r u", g=PASSES, u=K_PAIRS),
-                in_=h_t[:].rearrange("p g u r -> p g r u"),
+                in_=h_planes[b, s][:].rearrange("p g u r -> p g r u"),
             )
+            h_words[b, s] = h_grouped
+
+        def quantise_h(b, s):
+            i = b * SUB + s
             cols = slice(i * PASSES * P, (i + 1) * PASSES * P)
             nc.vector.quantize_mx(
-                out=h_codes[:, cols].bitcast(FP8X4),
-                scales=h_scales[:, cols],
-                in_=h_grouped[:],
+                out=h_codes[:, cols].bitcast(FP8X4), scales=h_scales[:, cols], in_=h_words[b, s][:]
             )
 
-        w_codes = [resident.tile([P, PASSES, QD], U32, name="w_codes%d" % m, align_bytes=64) for m in range(3)]
-        w_scales = [resident.tile([P, PASSES, QD], U8, name="w_scales%d" % m, align_bytes=64) for m in range(3)]
+        w_codes = [resident.tile([P, N_CHUNKS, PASSES, N_TILE], U32, name="w_codes%d" % m, align_bytes=64) for m in range(3)]
+        w_scales = [resident.tile([P, N_CHUNKS, PASSES, N_TILE], U8, name="w_scales%d" % m, align_bytes=64) for m in range(3)]
+        w_words = {}
 
-        def quantise_weight_chunk(m, c, copy):
-            cols = slice(c * N_TILE, (c + 1) * N_TILE)
-            grouped = []
-            for g in range(PASSES):
-                w_grouped = w_grouped_pool.tile([P, N_TILE, PACK], BF16, align_bytes=64)
-                copy(
-                    out=w_grouped[:].rearrange("p (a i) t -> p a t i", i=4),
-                    in_=w_raw[m][g][:, :, cols].rearrange("p t (a i) -> p a t i", i=4),
-                )
-                grouped.append(w_grouped)
-            for g in range(PASSES):
-                nc.vector.quantize_mx(
-                    out=w_codes[m][:, g, cols].bitcast(FP8X4),
-                    scales=w_scales[m][:, g, cols],
-                    in_=grouped[g][:].rearrange("p n t -> p (n t)"),
-                )
+        def group_weight(m, c, g, engine):
+            if (m, c) not in w_words:
+                w_grouped = w_grouped_pool.tile([P, PASSES, N_TILE, PACK], BF16, align_bytes=64)
+                w_words[m, c] = w_grouped
+            src = wq_raw[c][:, g, :, :] if m == Q else w_raw[m - K][g][:, :, c * N_TILE : (c + 1) * N_TILE]
+            out = w_words[m, c][:, g, :, :].rearrange("p (a i) t -> p a t i", i=4)
+            src = src.rearrange("p t (a i) -> p a t i", i=4)
+            if engine == "scalar":
+                nc.scalar.copy(out=out, in_=src)
+            else:
+                nc.vector.tensor_copy(out=out, in_=src)
 
-        def project(m, b, s, c):
+        def quantise_weight(m, c):
+            nc.vector.quantize_mx(
+                out=w_codes[m][:, c, :, :].rearrange("p g n -> p (g n)").bitcast(FP8X4),
+                scales=w_scales[m][:, c, :, :].rearrange("p g n -> p (g n)"),
+                in_=w_words[m, c][:].rearrange("p g n t -> p (g n t)"),
+            )
+
+        def project(m, b, s, c, acc):
             i = b * SUB + s
-            cols = slice(c * N_TILE, (c + 1) * N_TILE)
-            acc = psum.tile([P, N_TILE], F32, tag="acc")
             for g in range(PASSES):
                 tokens = slice((i * PASSES + g) * P, (i * PASSES + g + 1) * P)
                 nc.tensor.matmul_mx(
                     out=acc[:],
                     lhsT=h_codes[:, tokens].bitcast(FP8X4),
                     lhsT_scale=h_scales[:, tokens],
-                    rhs=w_codes[m][:, g, cols].bitcast(FP8X4),
-                    rhs_scale=w_scales[m][:, g, cols],
+                    rhs=w_codes[m][:, c, g, :].bitcast(FP8X4),
+                    rhs_scale=w_scales[m][:, c, g, :],
                     start=(g == 0),
                     stop=(g == PASSES - 1),
                 )
-            return acc
 
         rot_shape = [P, N_HEADS, PAIRS, 2]
 
-        def rotate(acc, s, y):
-            by_parity = acc[:].rearrange("p (h j e) -> p e h j", j=PAIRS, e=2)
-            share = []
-            for parity in (EVEN, ODD):
-                product = rot_pool.tile(rot_shape, F32, name="share%d" % parity)
+        def rotate(acc, s, y, adder):
+            u = acc[:].rearrange("p (h j r) -> p h j r", j=PAIRS, r=2)
+            direct = rot_pool.tile(rot_shape, F32)
+            crossed = rot_pool.tile(rot_shape, F32)
+            for product, factor, table in ((direct, u, cos_table), (crossed, u[:, :, :, ::-1], sin_table)):
                 nc.vector.tensor_tensor(
                     out=product[:],
-                    in0=by_parity[:, parity, :, :].unsqueeze(3).to_broadcast(rot_shape),
-                    in1=factors[:, s, parity, :, :].unsqueeze(1).to_broadcast(rot_shape),
+                    in0=factor,
+                    in1=table[:, s, :, :].unsqueeze(1).to_broadcast(rot_shape),
                     op=ALU.mult,
                 )
-                share.append(product)
-            nc.gpsimd.tensor_tensor(
+            adder.tensor_tensor(
                 out=y,
-                in0=share[EVEN][:].rearrange("p h j r -> p h (j r)"),
-                in1=share[ODD][:].rearrange("p h j r -> p h (j r)"),
+                in0=direct[:].rearrange("p h j r -> p h (j r)"),
+                in1=crossed[:].rearrange("p h j r -> p h (j r)"),
                 op=ALU.add,
             )
 
-        def new_result():
-            y_tile = y_pool.tile([P, N_HEADS, SUB, HEAD_DIM], F32)
-            return y_tile
+        results = {}
 
-        def store(m, b, c, y_tile):
+        def result(m, b, c):
+            if (m, b, c) not in results:
+                y_tile = y_pool.tile([P, N_HEADS, SUB, HEAD_DIM], F32)
+                results[m, b, c] = y_tile
+            return results[m, b, c]
+
+        def store(m, b, c, s0, s1):
             heads = slice(c * N_HEADS, (c + 1) * N_HEADS)
             nc.sync.dma_start(
-                out=outs[m][b, heads, :, :].rearrange("h (p s) d -> p h (s d)", s=SUB),
-                in_=y_tile[:].rearrange("p h s d -> p h (s d)"),
+                out=outs[m][b, heads, :, :].rearrange("h (p s) d -> p h s d", s=SUB)[:, :, s0:s1, :].rearrange("p h s d -> p h (s d)"),
+                in_=results[m, b, c][:, :, s0:s1, :].rearrange("p h s d -> p h (s d)"),
             )
 
-        def rotated_unit(m, b, s, c, y_tile):
-            rotate(project(m, b, s, c), s, y_tile[:, :, s, :])
+        def plain_unit(b, s, c):
+            acc = psum_aux.tile([P, N_TILE], F32, tag="aux")
+            project(V, b, s, c, acc)
+            nc.scalar.copy(out=result(V, b, c)[:, :, s, :], in_=acc[:].rearrange("p (h d) -> p h d", d=HEAD_DIM))
 
-        def plain_unit(m, b, s, c, y_tile):
-            acc = project(m, b, s, c)
-            nc.scalar.copy(out=y_tile[:, :, s, :], in_=acc[:].rearrange("p (h d) -> p h d", d=HEAD_DIM))
+        make_turns()
+        shift_turns()
+        round_off(whole[:], turns[:])
+        round_off(whole_shifted[:], shifted[:])
+        make_sin_turns()
+        make_cos_turns()
+        square(0, 0)
+        square(0, 1)
+        normalise(0, 0)
+        square(0, 2)
+        normalise(0, 1)
+        group_h(0, 0)
+        square(0, 3)
+        normalise(0, 2)
+        group_h(0, 1)
+        quantise_h(0, 0)
+        group_weight(Q, 0, 0, "vector")
+        normalise(0, 3)
+        group_h(0, 2)
+        quantise_h(0, 1)
+        group_weight(Q, 0, 1, "scalar")
+        quantise_h(0, 2)
+        group_h(0, 3)
+        make_tables()
+        quantise_weight(Q, 0)
+        quantise_h(0, 3)
+        group_weight(Q, 1, 0, "scalar")
+        group_weight(Q, 1, 1, "scalar")
+        for s in range(SUB):
+            square(1, s)
 
+        side = {}
+
+        def after(i, f, *args):
+            side.setdefault(i, []).append((f, args))
+
+        after(0, quantise_weight, Q, 1)
+        regroupings = [(m, c, g) for m, c in ((K, 0), (V, 0), (K, 1), (V, 1)) for g in range(PASSES)]
         for s in range(SUB):
-            quantise_token_tile(0, s)
-        for c in range(N_CHUNKS):
-            quantise_weight_chunk(Q, c, nc.vector.tensor_copy)
-        for c in range(N_CHUNKS):
-            y_q = new_result()
-            for s in range(SUB):
-                rotated_unit(Q, 0, s, c, y_q)
-            store(Q, 0, c, y_q)
-        for s in range(SUB):
-            quantise_token_tile(1, s)
-        for c in range(N_CHUNKS):
-            y_q = new_result()
-            for s in range(SUB):
-                rotated_unit(Q, 1, s, c, y_q)
-            store(Q, 1, c, y_q)
-        for c in range(N_CHUNKS):
-            quantise_weight_chunk(K, c, nc.scalar.copy)
-            quantise_weight_chunk(V, c, nc.scalar.copy)
-            for b in range(BATCH):
-                y_k = new_result()
-                y_v = new_result()
-                for s in range(SUB):
-                    rotated_unit(K, b, s, c, y_k)
-                    plain_unit(V, b, s, c, y_v)
-                store(V, b, c, y_v)
-                store(K, b, c, y_k)
+            after(1 + s, normalise, 1, s)
+            after(2 + s, group_h, 1, s)
+            after(3 + s, quantise_h, 1, s)
+        for i, (m, c, g) in enumerate(regroupings):
+            after(2 + i, group_weight, m, c, g, "scalar")
+        after(9, quantise_weight, K, 0)
+        after(11, quantise_weight, V, 0)
+        after(14, quantise_weight, K, 1)
+        after(16, quantise_weight, V, 1)
+        plain = [(b, s, c) for c in range(N_CHUNKS) for b in range(BATCH) for s in range(SUB)]
+        for n, (b, s, c) in enumerate(plain):
+            i = (14 if c == 0 else 19) + (n % 8) * 2 // 3
+            after(i, plain_unit, b, s, c)
+            if s == SUB - 1:
+                after(i, store, V, b, c, 0, SUB)
+
+        groups = [(Q, 0, 0), (Q, 0, 1), (Q, 1, 0), (Q, 1, 1), (K, 0, 0), (K, 1, 0), (K, 0, 1), (K, 1, 1)]
+        rotations = [(m, b, s, c) for m, b, c in groups for s in range(SUB)]
+        banks = {}
+
+        def start_rotation(i):
+            if i < len(rotations):
+                acc = psum.tile([P, N_TILE], F32, tag="acc")
+                project(*rotations[i], acc)
+                banks[i] = acc
+
+        for i in range(LOOKAHEAD):
+            start_rotation(i)
+        for i, (m, b, s, c) in enumerate(rotations):
+            start_rotation(i + LOOKAHEAD)
+            adder = nc.vector if i in (len(rotations) - 3, len(rotations) - 1) else nc.gpsimd
+            rotate(banks[i], s, result(m, b, c)[:, :, s, :], adder)
+            if i >= len(rotations) - SUB:
+                store(m, b, c, s, s + 1)
+            elif s == SUB - 1:
+                store(m, b, c, 0, SUB)
+            for f, args in side.get(i, []):
+                f(*args)

@@ -33,6 +33,7 @@ N_HEADS = N_TILE // HEAD_DIM
 N_CHUNKS = QD // N_TILE
 K_PAIRS = PACK // 2
 
+VECTOR_SUMS = (29, 31)
 LOOKAHEAD = 2
 
 ROUND_MAGIC = 12582912.0
@@ -51,12 +52,14 @@ def tile_flexattentionblock_pa_kernel(tc, x, attn_norm_w, wq, wk, wv, out_0, out
         resident = ctx.enter_context(tc.tile_pool(name="resident", bufs=1))
         squares_pool = ctx.enter_context(tc.tile_pool(name="squares", bufs=2))
         h_pool = ctx.enter_context(tc.tile_pool(name="h", bufs=4))
-        w_grouped_pool = ctx.enter_context(tc.tile_pool(name="w_grouped", bufs=3))
+        w_grouped_pool = ctx.enter_context(tc.tile_pool(name="w_grouped", bufs=4))
         rot_pool = ctx.enter_context(tc.tile_pool(name="rot", bufs=4))
-        y_pool = ctx.enter_context(tc.tile_pool(name="y", bufs=5))
+        y_pool = ctx.enter_context(tc.tile_pool(name="y", bufs=4))
+        last_pool = ctx.enter_context(tc.tile_pool(name="last", bufs=SUB))
         psum_gain = ctx.enter_context(tc.psum_pool(name="psum_gain", bufs=1))
+        psum_sum = ctx.enter_context(tc.psum_pool(name="psum_sum", bufs=2))
         psum_aux = ctx.enter_context(tc.psum_pool(name="psum_aux", bufs=2))
-        psum = ctx.enter_context(tc.psum_pool(name="psum", bufs=4))
+        psum = ctx.enter_context(tc.psum_pool(name="psum", bufs=3))
         ctx.enter_context(tc.manual_schedule())
 
         sin_probe = const.tile([P, 1], F32)
@@ -92,8 +95,8 @@ def tile_flexattentionblock_pa_kernel(tc, x, attn_norm_w, wq, wk, wv, out_0, out
         for s in range(1, SUB):
             load_x(0, s)
         load_wq(0)
-        load_wq(1)
         nc.sync.dma_start(out=x_sb[1][:], in_=x[1, :, :].rearrange("(p s) k -> p s k", s=SUB))
+        load_wq(1)
         load_weight(K)
         load_weight(V)
 
@@ -104,13 +107,10 @@ def tile_flexattentionblock_pa_kernel(tc, x, attn_norm_w, wq, wk, wv, out_0, out
         neg_half = const.tile([P, 1], F32)
         nc.gpsimd.memset(neg_half[:], -0.5)
 
-        gain = []
+        gain = psum_gain.tile([P, DIM], BF16)
         for half in range(DIM // N_TILE):
-            spread = psum_gain.tile([P, N_TILE], F32, name="gain%d" % half)
-            nc.tensor.matmul(
-                out=spread[:], lhsT=ones[:], rhs=gain_row[:, half * N_TILE : (half + 1) * N_TILE], start=True, stop=True
-            )
-            gain.append(spread)
+            cols = slice(half * N_TILE, (half + 1) * N_TILE)
+            nc.tensor.matmul(out=gain[:, cols], lhsT=ones[:], rhs=gain_row[:, cols], start=True, stop=True)
 
         freq = const.tile([P, PAIRS], F32)
         pos_int = const.tile([P, SUB], I32)
@@ -160,17 +160,23 @@ def tile_flexattentionblock_pa_kernel(tc, x, attn_norm_w, wq, wk, wv, out_0, out
         def make_cos_turns():
             nc.vector.tensor_tensor(out=cos_turns[:], in0=shifted[:], in1=whole_shifted[:], op=ALU.subtract)
 
+        mixed_table = const.tile(pair_shape, F32)
+
         def make_tables():
             nc.scalar.activation(out=sin_table[:], in_=sin_turns[:], func=ACT.Sin, scale=2.0 * math.pi)
             nc.scalar.activation(
                 out=cos_table[:], in_=cos_turns[:].unsqueeze(3).to_broadcast(pair_shape), func=ACT.Sin, scale=2.0 * math.pi
             )
 
+        def make_mixed_table():
+            nc.gpsimd.tensor_tensor(out=mixed_table[:], in0=sin_table[:], in1=cos_table[:], op=ALU.subtract)
+
         h_codes = resident.tile([P, BATCH * SUB * PASSES * P], U32, align_bytes=64)
         h_scales = resident.tile([P, BATCH * SUB * PASSES * P], U8, align_bytes=64)
         mean_sq = const.tile([P, BATCH * SUB], F32)
         mean_eps = const.tile([P, BATCH * SUB], F32)
         rstd = const.tile([P, BATCH * SUB], F32)
+        ready = set()
         h_planes = {}
         h_words = {}
 
@@ -186,16 +192,9 @@ def tile_flexattentionblock_pa_kernel(tc, x, attn_norm_w, wq, wk, wv, out_0, out
         def normalise(b, s):
             one = slice(b * SUB + s, b * SUB + s + 1)
             h = h_pool.tile([P, DIM], BF16)
-            for half in range(DIM // N_TILE):
-                cols = slice(half * N_TILE, (half + 1) * N_TILE)
-                nc.vector.scalar_tensor_tensor(
-                    out=h[:, cols],
-                    in0=x_sb[b][:, s, cols],
-                    scalar=rstd[:, one],
-                    in1=gain[half][:],
-                    op0=ALU.mult,
-                    op1=ALU.mult,
-                )
+            nc.vector.scalar_tensor_tensor(
+                out=h[:], in0=x_sb[b][:, s, :], scalar=rstd[:, one], in1=gain[:], op0=ALU.mult, op1=ALU.mult
+            )
             words = h[:].bitcast(F32)
             h_t = psum_aux.tile([P, PASSES, K_PAIRS, P], F32, tag="aux")
             for g in range(PASSES):
@@ -219,22 +218,27 @@ def tile_flexattentionblock_pa_kernel(tc, x, attn_norm_w, wq, wk, wv, out_0, out
             nc.vector.quantize_mx(
                 out=h_codes[:, cols].bitcast(FP8X4), scales=h_scales[:, cols], in_=h_words[b, s][:]
             )
+            ready.add(("h", b, s))
 
         w_codes = [resident.tile([P, N_CHUNKS, PASSES, N_TILE], U32, name="w_codes%d" % m, align_bytes=64) for m in range(3)]
         w_scales = [resident.tile([P, N_CHUNKS, PASSES, N_TILE], U8, name="w_scales%d" % m, align_bytes=64) for m in range(3)]
         w_words = {}
+        SPLIT = (Q,)
 
         def group_weight(m, c, g, engine):
             if (m, c) not in w_words:
                 w_grouped = w_grouped_pool.tile([P, PASSES, N_TILE, PACK], BF16, align_bytes=64)
                 w_words[m, c] = w_grouped
             src = wq_raw[c][:, g, :, :] if m == Q else w_raw[m - K][g][:, :, c * N_TILE : (c + 1) * N_TILE]
-            out = w_words[m, c][:, g, :, :].rearrange("p (a i) t -> p a t i", i=4)
-            src = src.rearrange("p t (a i) -> p a t i", i=4)
-            if engine == "scalar":
-                nc.scalar.copy(out=out, in_=src)
-            else:
-                nc.vector.tensor_copy(out=out, in_=src)
+            copy = nc.scalar.copy if engine == "scalar" else nc.vector.tensor_copy
+            step = 2 if m in SPLIT else 1
+            width = N_TILE // step
+            for e in range(step):
+                out = w_words[m, c][:, g, e * width : (e + 1) * width, :]
+                copy(
+                    out=out.rearrange("p (a i) t -> p a t i", i=4),
+                    in_=src[:, :, e::step].rearrange("p t (a i) -> p a t i", i=4),
+                )
 
         def quantise_weight(m, c):
             nc.vector.quantize_mx(
@@ -242,6 +246,7 @@ def tile_flexattentionblock_pa_kernel(tc, x, attn_norm_w, wq, wk, wv, out_0, out
                 scales=w_scales[m][:, c, :, :].rearrange("p g n -> p (g n)"),
                 in_=w_words[m, c][:].rearrange("p g n t -> p (g n t)"),
             )
+            ready.add(("w", m, c))
 
         def project(m, b, s, c, acc):
             i = b * SUB + s
@@ -261,8 +266,8 @@ def tile_flexattentionblock_pa_kernel(tc, x, attn_norm_w, wq, wk, wv, out_0, out
 
         def rotate(acc, s, y, adder):
             u = acc[:].rearrange("p (h j r) -> p h j r", j=PAIRS, r=2)
-            direct = rot_pool.tile(rot_shape, F32)
-            crossed = rot_pool.tile(rot_shape, F32)
+            direct = rot_pool.tile(rot_shape, F32, tag="direct")
+            crossed = rot_pool.tile(rot_shape, F32, tag="crossed")
             for product, factor, table in ((direct, u, cos_table), (crossed, u[:, :, :, ::-1], sin_table)):
                 nc.vector.tensor_tensor(
                     out=product[:],
@@ -277,6 +282,50 @@ def tile_flexattentionblock_pa_kernel(tc, x, attn_norm_w, wq, wk, wv, out_0, out
                 op=ALU.add,
             )
 
+        def project_sum(b, s, c, acc):
+            i = b * SUB + s
+            half = N_TILE // 2
+            for g in range(PASSES):
+                tokens = slice((i * PASSES + g) * P, (i * PASSES + g + 1) * P)
+                for e in range(2):
+                    cols = slice(e * half, (e + 1) * half)
+                    nc.tensor.matmul_mx(
+                        out=acc,
+                        lhsT=h_codes[:, tokens].bitcast(FP8X4),
+                        lhsT_scale=h_scales[:, tokens],
+                        rhs=w_codes[Q][:, c, g, cols].bitcast(FP8X4),
+                        rhs_scale=w_scales[Q][:, c, g, cols],
+                        start=(g == 0 and e == 0),
+                        stop=(g == PASSES - 1 and e == 1),
+                    )
+
+        def rotate_pair(accs, sums, s0, ys, adder):
+            crossed = []
+            for n in range(2):
+                product = rot_pool.tile(rot_shape, F32, tag="crossed")
+                nc.vector.tensor_tensor(
+                    out=product[:],
+                    in0=accs[n][:].rearrange("p (r h j) -> p h j r", r=2, j=PAIRS)[:, :, :, ::-1],
+                    in1=mixed_table[:, s0 + n, :, :].unsqueeze(1).to_broadcast(rot_shape),
+                    op=ALU.mult,
+                )
+                crossed.append(product)
+            common_shape = [P, 2, N_HEADS, PAIRS]
+            common = rot_pool.tile(common_shape, F32, tag="direct")
+            nc.vector.tensor_tensor(
+                out=common[:],
+                in0=sums[:].rearrange("p n (h j) -> p n h j", j=PAIRS),
+                in1=cos_table[:, s0 : s0 + 2, :, 0].unsqueeze(2).to_broadcast(common_shape),
+                op=ALU.mult,
+            )
+            for n in range(2):
+                adder[n].tensor_tensor(
+                    out=ys[n].rearrange("p h (j r) -> p h j r", r=2),
+                    in0=common[:, n, :, :].unsqueeze(3).to_broadcast(rot_shape),
+                    in1=crossed[n][:],
+                    op=ALU.add,
+                )
+
         results = {}
 
         def result(m, b, c):
@@ -285,11 +334,17 @@ def tile_flexattentionblock_pa_kernel(tc, x, attn_norm_w, wq, wk, wv, out_0, out
                 results[m, b, c] = y_tile
             return results[m, b, c]
 
-        def store(m, b, c, s0, s1):
+        def store(m, b, c):
             heads = slice(c * N_HEADS, (c + 1) * N_HEADS)
             nc.sync.dma_start(
-                out=outs[m][b, heads, :, :].rearrange("h (p s) d -> p h s d", s=SUB)[:, :, s0:s1, :].rearrange("p h s d -> p h (s d)"),
-                in_=results[m, b, c][:, :, s0:s1, :].rearrange("p h s d -> p h (s d)"),
+                out=outs[m][b, heads, :, :].rearrange("h (p s) d -> p h (s d)", s=SUB),
+                in_=results[m, b, c][:].rearrange("p h s d -> p h (s d)"),
+            )
+
+        def store_tile(m, b, s, c, y_tile):
+            heads = slice(c * N_HEADS, (c + 1) * N_HEADS)
+            nc.sync.dma_start(
+                out=outs[m][b, heads, :, :].rearrange("h (p s) d -> p h s d", s=SUB)[:, :, s, :], in_=y_tile[:]
             )
 
         def plain_unit(b, s, c):
@@ -303,74 +358,104 @@ def tile_flexattentionblock_pa_kernel(tc, x, attn_norm_w, wq, wk, wv, out_0, out
         round_off(whole_shifted[:], shifted[:])
         make_sin_turns()
         make_cos_turns()
-        square(0, 0)
-        square(0, 1)
-        normalise(0, 0)
-        square(0, 2)
-        normalise(0, 1)
-        group_h(0, 0)
-        square(0, 3)
-        normalise(0, 2)
-        group_h(0, 1)
-        quantise_h(0, 0)
-        group_weight(Q, 0, 0, "vector")
-        normalise(0, 3)
-        group_h(0, 2)
-        quantise_h(0, 1)
-        group_weight(Q, 0, 1, "scalar")
-        quantise_h(0, 2)
-        group_h(0, 3)
-        make_tables()
-        quantise_weight(Q, 0)
-        quantise_h(0, 3)
-        group_weight(Q, 1, 0, "scalar")
-        group_weight(Q, 1, 1, "scalar")
         for s in range(SUB):
-            square(1, s)
+            square(0, s)
+        make_tables()
+        make_mixed_table()
+        for s in range(SUB):
+            normalise(0, s)
+            if s < 2:
+                group_h(0, s)
+        group_weight(Q, 0, 0, "vector")
+        group_weight(Q, 0, 1, "scalar")
+        quantise_h(0, 0)
+        quantise_h(0, 1)
+        quantise_weight(Q, 0)
+        for s in (2, 3):
+            group_h(0, s)
+            quantise_h(0, s)
+        square(1, 0)
+        square(1, 1)
+        group_weight(Q, 1, 0, "scalar")
 
         side = {}
 
         def after(i, f, *args):
             side.setdefault(i, []).append((f, args))
 
-        after(0, quantise_weight, Q, 1)
-        regroupings = [(m, c, g) for m, c in ((K, 0), (V, 0), (K, 1), (V, 1)) for g in range(PASSES)]
-        for s in range(SUB):
-            after(1 + s, normalise, 1, s)
-            after(2 + s, group_h, 1, s)
-            after(3 + s, quantise_h, 1, s)
+        regroupings = [(m, c, g) for m, c in ((V, 0), (K, 1), (V, 1)) for g in range(PASSES)]
+        after(1, normalise, 1, 0)
+        after(1, square, 1, 2)
+        after(1, group_h, 1, 0)
+        after(1, normalise, 1, 1)
+        after(1, square, 1, 3)
+        after(1, group_h, 1, 1)
+        after(1, group_weight, Q, 1, 1, "scalar")
+        after(3, normalise, 1, 2)
+        after(3, normalise, 1, 3)
+        after(3, quantise_h, 1, 0)
+        after(3, quantise_h, 1, 1)
+        after(3, group_h, 1, 2)
+        after(3, quantise_weight, Q, 1)
+        after(3, group_weight, K, 0, 0, "scalar")
+        after(3, group_h, 1, 3)
+        after(3, group_weight, K, 0, 1, "scalar")
+        after(5, quantise_h, 1, 2)
+        after(5, quantise_h, 1, 3)
         for i, (m, c, g) in enumerate(regroupings):
-            after(2 + i, group_weight, m, c, g, "scalar")
-        after(9, quantise_weight, K, 0)
-        after(11, quantise_weight, V, 0)
-        after(14, quantise_weight, K, 1)
-        after(16, quantise_weight, V, 1)
+            after(7 + 2 * (i // 2), group_weight, m, c, g, "scalar")
+        after(11, quantise_weight, K, 0)
+        after(13, quantise_weight, V, 0)
+        after(17, quantise_weight, K, 1)
+        after(19, quantise_weight, V, 1)
         plain = [(b, s, c) for c in range(N_CHUNKS) for b in range(BATCH) for s in range(SUB)]
         for n, (b, s, c) in enumerate(plain):
-            i = (14 if c == 0 else 19) + (n % 8) * 2 // 3
+            i = 15 + n * 2 // 3
             after(i, plain_unit, b, s, c)
             if s == SUB - 1:
-                after(i, store, V, b, c, 0, SUB)
+                after(i, store, V, b, c)
 
         groups = [(Q, 0, 0), (Q, 0, 1), (Q, 1, 0), (Q, 1, 1), (K, 0, 0), (K, 1, 0), (K, 0, 1), (K, 1, 1)]
         rotations = [(m, b, s, c) for m, b, c in groups for s in range(SUB)]
         banks = {}
+        started = []
 
-        def start_rotation(i):
-            if i < len(rotations):
+        def start_rotations(end):
+            for i in range(len(started), min(end, len(rotations))):
+                m, b, s, c = rotations[i]
+                if ("h", b, s) not in ready or ("w", m, c) not in ready:
+                    break
                 acc = psum.tile([P, N_TILE], F32, tag="acc")
-                project(*rotations[i], acc)
+                project(m, b, s, c, acc)
                 banks[i] = acc
+                started.append(i)
+                if m in SPLIT and s % 2 == 1:
+                    sums = psum_sum.tile([P, 2, N_TILE // 2], F32)
+                    for n in range(2):
+                        project_sum(b, s - 1 + n, c, sums[:, n, :])
+                    banks[i, "sum"] = sums
 
-        for i in range(LOOKAHEAD):
-            start_rotation(i)
+        start_rotations(2)
         for i, (m, b, s, c) in enumerate(rotations):
-            start_rotation(i + LOOKAHEAD)
-            adder = nc.vector if i in (len(rotations) - 3, len(rotations) - 1) else nc.gpsimd
-            rotate(banks[i], s, result(m, b, c)[:, :, s, :], adder)
-            if i >= len(rotations) - SUB:
-                store(m, b, c, s, s + 1)
-            elif s == SUB - 1:
-                store(m, b, c, 0, SUB)
+            if i < len(rotations) - SUB:
+                y = result(m, b, c)
+            adder = nc.vector if i in VECTOR_SUMS else nc.gpsimd
+            if m not in SPLIT:
+                start_rotations(i + LOOKAHEAD + 1)
+                if i < len(rotations) - SUB:
+                    rotate(banks[i], s, y[:, :, s, :], adder)
+                else:
+                    y_last = last_pool.tile([P, N_HEADS, HEAD_DIM], F32)
+                    rotate(banks[i], s, y_last[:], adder)
+                    store_tile(m, b, s, c, y_last)
+            elif s % 2 == 1:
+                start_rotations(i + 3)
+                rotate_pair(
+                    [banks[i - 1], banks[i]], banks[i, "sum"], s - 1, [y[:, :, s - 1, :], y[:, :, s, :]],
+                    [nc.gpsimd, nc.gpsimd],
+                )
+            if s == SUB - 1 and i < len(rotations) - SUB:
+                store(m, b, c)
             for f, args in side.get(i, []):
                 f(*args)
+                start_rotations(i + 3)

@@ -34,7 +34,7 @@ N_CHUNKS = QD // N_TILE
 K_PAIRS = PACK // 2
 
 VECTOR_SUMS = (29, 31)
-LOOKAHEAD = 2
+LOOKAHEAD = 3
 
 ROUND_MAGIC = 12582912.0
 
@@ -57,14 +57,17 @@ def tile_flexattentionblock_pa_kernel(tc, x, attn_norm_w, wq, wk, wv, out_0, out
         y_pool = ctx.enter_context(tc.tile_pool(name="y", bufs=4))
         last_pool = ctx.enter_context(tc.tile_pool(name="last", bufs=SUB))
         psum_gain = ctx.enter_context(tc.psum_pool(name="psum_gain", bufs=1))
-        psum_sum = ctx.enter_context(tc.psum_pool(name="psum_sum", bufs=2))
         psum_aux = ctx.enter_context(tc.psum_pool(name="psum_aux", bufs=2))
-        psum = ctx.enter_context(tc.psum_pool(name="psum", bufs=3))
+        psum = ctx.enter_context(tc.psum_pool(name="psum", bufs=5))
         ctx.enter_context(tc.manual_schedule())
 
         sin_probe = const.tile([P, 1], F32)
         nc.vector.memset(sin_probe[:], 0.0)
         nc.scalar.activation(out=sin_probe[:], in_=sin_probe[:], func=ACT.Sin)
+        ones = const.tile([P, P], BF16)
+        nc.vector.memset(ones[:], 1.0)
+        pos_int = const.tile([P, SUB], I32)
+        nc.gpsimd.iota(pos_int[:], pattern=[[1, SUB]], base=0, channel_multiplier=SUB)
 
         gain_row = const.tile([P, DIM], BF16)
         nc.gpsimd.memset(gain_row[:].bitcast(I32), 0)
@@ -100,10 +103,10 @@ def tile_flexattentionblock_pa_kernel(tc, x, attn_norm_w, wq, wk, wv, out_0, out
         load_weight(K)
         load_weight(V)
 
+        ident_bf16 = const.tile([P, P], BF16)
+        make_identity(nc, ident_bf16[:])
         ident = const.tile([P, P], F32)
         make_identity(nc, ident[:])
-        ones = const.tile([P, P], BF16)
-        nc.gpsimd.memset(ones[:], 1.0)
         neg_half = const.tile([P, 1], F32)
         nc.gpsimd.memset(neg_half[:], -0.5)
 
@@ -112,64 +115,44 @@ def tile_flexattentionblock_pa_kernel(tc, x, attn_norm_w, wq, wk, wv, out_0, out
             cols = slice(half * N_TILE, (half + 1) * N_TILE)
             nc.tensor.matmul(out=gain[:, cols], lhsT=ones[:], rhs=gain_row[:, cols], start=True, stop=True)
 
-        freq = const.tile([P, PAIRS], F32)
-        pos_int = const.tile([P, SUB], I32)
-        pos = const.tile([P, SUB], F32)
         table_shape = [P, SUB, PAIRS]
         pair_shape = [P, SUB, PAIRS, 2]
         turns = const.tile(table_shape, F32)
         whole = const.tile(table_shape, F32)
-        shifted = const.tile(table_shape, F32)
-        whole_shifted = const.tile(table_shape, F32)
-        cos_turns = const.tile(table_shape, F32)
         sin_turns = const.tile(pair_shape, F32)
+        size_turns = const.tile(table_shape, F32)
         cos_table = const.tile(pair_shape, F32)
         sin_table = const.tile(pair_shape, F32)
 
         def make_turns():
-            nc.gpsimd.iota(pos_int[:], pattern=[[1, SUB]], base=0, channel_multiplier=SUB)
-            nc.vector.memset(freq[:, 0:1], 1.0)
+            nc.vector.tensor_scalar_mul(out=turns[:, :, 0], in0=pos_int[:], scalar1=1.0 / (2.0 * math.pi))
             width = 1
             while width < PAIRS:
-                nc.vector.tensor_scalar_mul(
-                    out=freq[:, width : 2 * width], in0=freq[:, 0:width], scalar1=THETA ** (-2.0 * width / HEAD_DIM)
-                )
-                width *= 2
-            nc.vector.tensor_copy(out=pos[:], in_=pos_int[:])
-            nc.vector.scalar_tensor_tensor(
-                out=turns[:],
-                in0=freq[:].unsqueeze(1).to_broadcast(table_shape),
-                scalar=1.0 / (2.0 * math.pi),
-                in1=pos[:].unsqueeze(2).to_broadcast(table_shape),
-                op0=ALU.mult,
-                op1=ALU.mult,
-            )
-
-        def round_off(out, in_):
+                for n in range(1, 4):
+                    nc.vector.tensor_scalar_mul(
+                        out=turns[:, :, n * width : (n + 1) * width],
+                        in0=turns[:, :, 0:width],
+                        scalar1=THETA ** (-2.0 * n * width / HEAD_DIM),
+                    )
+                width *= 4
             nc.vector.tensor_scalar(
-                out=out, in0=in_, scalar1=ROUND_MAGIC, scalar2=ROUND_MAGIC, op0=ALU.add, op1=ALU.subtract
+                out=whole[:], in0=turns[:], scalar1=ROUND_MAGIC, scalar2=ROUND_MAGIC, op0=ALU.add, op1=ALU.subtract
             )
-
-        def make_sin_turns():
             nc.vector.tensor_tensor(out=sin_turns[:, :, :, 1], in0=turns[:], in1=whole[:], op=ALU.subtract)
             nc.vector.tensor_tensor(out=sin_turns[:, :, :, 0], in0=whole[:], in1=turns[:], op=ALU.subtract)
-
-        def shift_turns():
-            nc.vector.tensor_scalar_add(out=shifted[:], in0=turns[:], scalar1=0.25)
-
-        def make_cos_turns():
-            nc.vector.tensor_tensor(out=cos_turns[:], in0=shifted[:], in1=whole_shifted[:], op=ALU.subtract)
-
-        mixed_table = const.tile(pair_shape, F32)
+            nc.vector.tensor_tensor(
+                out=size_turns[:], in0=sin_turns[:, :, :, 0], in1=sin_turns[:, :, :, 1], op=ALU.max
+            )
 
         def make_tables():
             nc.scalar.activation(out=sin_table[:], in_=sin_turns[:], func=ACT.Sin, scale=2.0 * math.pi)
             nc.scalar.activation(
-                out=cos_table[:], in_=cos_turns[:].unsqueeze(3).to_broadcast(pair_shape), func=ACT.Sin, scale=2.0 * math.pi
+                out=cos_table[:],
+                in_=size_turns[:].unsqueeze(3).to_broadcast(pair_shape),
+                func=ACT.Sin,
+                scale=-2.0 * math.pi,
+                bias=math.pi / 2.0,
             )
-
-        def make_mixed_table():
-            nc.gpsimd.tensor_tensor(out=mixed_table[:], in0=sin_table[:], in1=cos_table[:], op=ALU.subtract)
 
         h_codes = resident.tile([P, BATCH * SUB * PASSES * P], U32, align_bytes=64)
         h_scales = resident.tile([P, BATCH * SUB * PASSES * P], U8, align_bytes=64)
@@ -179,6 +162,7 @@ def tile_flexattentionblock_pa_kernel(tc, x, attn_norm_w, wq, wk, wv, out_0, out
         ready = set()
         h_planes = {}
         h_words = {}
+        h_batch = const.tile([P, SUB * DIM], BF16, align_bytes=64)
 
         def square(b, s):
             one = slice(b * SUB + s, b * SUB + s + 1)
@@ -205,25 +189,30 @@ def tile_flexattentionblock_pa_kernel(tc, x, attn_norm_w, wq, wk, wv, out_0, out
             h_planes[b, s] = h_t
 
         def group_h(b, s):
-            h_grouped = h_pool.tile([P, PASSES * P * PACK], BF16, align_bytes=64)
+            if b == 0:
+                h_grouped = h_pool.tile([P, PASSES * P * PACK], BF16, align_bytes=64)
+                h_words[b, s] = h_grouped[:]
+            else:
+                h_words[b, s] = h_batch[:, s * DIM : (s + 1) * DIM]
             nc.scalar.copy(
-                out=h_grouped[:].bitcast(F32).rearrange("p (g r u) -> p g r u", g=PASSES, u=K_PAIRS),
+                out=h_words[b, s].bitcast(F32).rearrange("p (g r u) -> p g r u", g=PASSES, u=K_PAIRS),
                 in_=h_planes[b, s][:].rearrange("p g u r -> p g r u"),
             )
-            h_words[b, s] = h_grouped
 
-        def quantise_h(b, s):
+        def quantise_h(b, s, tiles=1):
             i = b * SUB + s
-            cols = slice(i * PASSES * P, (i + 1) * PASSES * P)
+            cols = slice(i * PASSES * P, (i + tiles) * PASSES * P)
             nc.vector.quantize_mx(
-                out=h_codes[:, cols].bitcast(FP8X4), scales=h_scales[:, cols], in_=h_words[b, s][:]
+                out=h_codes[:, cols].bitcast(FP8X4),
+                scales=h_scales[:, cols],
+                in_=h_words[b, s] if tiles == 1 else h_batch[:, s * DIM : (s + tiles) * DIM],
             )
-            ready.add(("h", b, s))
+            for n in range(tiles):
+                ready.add(("h", b, s + n))
 
         w_codes = [resident.tile([P, N_CHUNKS, PASSES, N_TILE], U32, name="w_codes%d" % m, align_bytes=64) for m in range(3)]
         w_scales = [resident.tile([P, N_CHUNKS, PASSES, N_TILE], U8, name="w_scales%d" % m, align_bytes=64) for m in range(3)]
         w_words = {}
-        SPLIT = (Q,)
 
         def group_weight(m, c, g, engine):
             if (m, c) not in w_words:
@@ -231,14 +220,35 @@ def tile_flexattentionblock_pa_kernel(tc, x, attn_norm_w, wq, wk, wv, out_0, out
                 w_words[m, c] = w_grouped
             src = wq_raw[c][:, g, :, :] if m == Q else w_raw[m - K][g][:, :, c * N_TILE : (c + 1) * N_TILE]
             copy = nc.scalar.copy if engine == "scalar" else nc.vector.tensor_copy
-            step = 2 if m in SPLIT else 1
-            width = N_TILE // step
-            for e in range(step):
-                out = w_words[m, c][:, g, e * width : (e + 1) * width, :]
-                copy(
-                    out=out.rearrange("p (a i) t -> p a t i", i=4),
-                    in_=src[:, :, e::step].rearrange("p t (a i) -> p a t i", i=4),
-                )
+            out = w_words[m, c][:, g, :, :]
+            copy(
+                out=out.rearrange("p (a i) t -> p a t i", i=4),
+                in_=src.rearrange("p t (a i) -> p a t i", i=4),
+            )
+
+        moved = {}
+
+        def move_weight(c, g):
+            half = N_TILE // 2
+            for a in range(2):
+                bank = psum.tile([P, half, PACK], BF16, tag="acc")
+                for t in range(0, PACK, 2):
+                    nc.tensor.matmul(
+                        out=bank[:, :, t : t + 2],
+                        lhsT=ident_bf16[:],
+                        rhs=wq_raw[c][:, g, t : t + 2, a * half : (a + 1) * half].rearrange("p t n -> p n t"),
+                        start=True,
+                        stop=True,
+                    )
+                moved[c, g, a] = bank
+
+        def take_weight(c, g, copy):
+            half = N_TILE // 2
+            if (Q, c) not in w_words:
+                w_grouped = w_grouped_pool.tile([P, PASSES, N_TILE, PACK], BF16, align_bytes=64)
+                w_words[Q, c] = w_grouped
+            for a in range(2):
+                copy(out=w_words[Q, c][:, g, a * half : (a + 1) * half, :], in_=moved[c, g, a][:])
 
         def quantise_weight(m, c):
             nc.vector.quantize_mx(
@@ -282,50 +292,6 @@ def tile_flexattentionblock_pa_kernel(tc, x, attn_norm_w, wq, wk, wv, out_0, out
                 op=ALU.add,
             )
 
-        def project_sum(b, s, c, acc):
-            i = b * SUB + s
-            half = N_TILE // 2
-            for g in range(PASSES):
-                tokens = slice((i * PASSES + g) * P, (i * PASSES + g + 1) * P)
-                for e in range(2):
-                    cols = slice(e * half, (e + 1) * half)
-                    nc.tensor.matmul_mx(
-                        out=acc,
-                        lhsT=h_codes[:, tokens].bitcast(FP8X4),
-                        lhsT_scale=h_scales[:, tokens],
-                        rhs=w_codes[Q][:, c, g, cols].bitcast(FP8X4),
-                        rhs_scale=w_scales[Q][:, c, g, cols],
-                        start=(g == 0 and e == 0),
-                        stop=(g == PASSES - 1 and e == 1),
-                    )
-
-        def rotate_pair(accs, sums, s0, ys, adder):
-            crossed = []
-            for n in range(2):
-                product = rot_pool.tile(rot_shape, F32, tag="crossed")
-                nc.vector.tensor_tensor(
-                    out=product[:],
-                    in0=accs[n][:].rearrange("p (r h j) -> p h j r", r=2, j=PAIRS)[:, :, :, ::-1],
-                    in1=mixed_table[:, s0 + n, :, :].unsqueeze(1).to_broadcast(rot_shape),
-                    op=ALU.mult,
-                )
-                crossed.append(product)
-            common_shape = [P, 2, N_HEADS, PAIRS]
-            common = rot_pool.tile(common_shape, F32, tag="direct")
-            nc.vector.tensor_tensor(
-                out=common[:],
-                in0=sums[:].rearrange("p n (h j) -> p n h j", j=PAIRS),
-                in1=cos_table[:, s0 : s0 + 2, :, 0].unsqueeze(2).to_broadcast(common_shape),
-                op=ALU.mult,
-            )
-            for n in range(2):
-                adder[n].tensor_tensor(
-                    out=ys[n].rearrange("p h (j r) -> p h j r", r=2),
-                    in0=common[:, n, :, :].unsqueeze(3).to_broadcast(rot_shape),
-                    in1=crossed[n][:],
-                    op=ALU.add,
-                )
-
         results = {}
 
         def result(m, b, c):
@@ -353,21 +319,18 @@ def tile_flexattentionblock_pa_kernel(tc, x, attn_norm_w, wq, wk, wv, out_0, out
             nc.scalar.copy(out=result(V, b, c)[:, :, s, :], in_=acc[:].rearrange("p (h d) -> p h d", d=HEAD_DIM))
 
         make_turns()
-        shift_turns()
-        round_off(whole[:], turns[:])
-        round_off(whole_shifted[:], shifted[:])
-        make_sin_turns()
-        make_cos_turns()
         for s in range(SUB):
             square(0, s)
-        make_tables()
-        make_mixed_table()
-        for s in range(SUB):
+        move_weight(0, 0)
+        normalise(0, 0)
+        move_weight(0, 1)
+        for s in range(1, SUB):
             normalise(0, s)
-            if s < 2:
-                group_h(0, s)
-        group_weight(Q, 0, 0, "vector")
-        group_weight(Q, 0, 1, "scalar")
+            if s < 3:
+                group_h(0, s - 1)
+        take_weight(0, 0, nc.vector.tensor_copy)
+        take_weight(0, 1, nc.scalar.copy)
+        make_tables()
         quantise_h(0, 0)
         quantise_h(0, 1)
         quantise_weight(Q, 0)
@@ -376,41 +339,41 @@ def tile_flexattentionblock_pa_kernel(tc, x, attn_norm_w, wq, wk, wv, out_0, out
             quantise_h(0, s)
         square(1, 0)
         square(1, 1)
-        group_weight(Q, 1, 0, "scalar")
 
         side = {}
 
         def after(i, f, *args):
             side.setdefault(i, []).append((f, args))
 
-        regroupings = [(m, c, g) for m, c in ((V, 0), (K, 1), (V, 1)) for g in range(PASSES)]
         after(1, normalise, 1, 0)
         after(1, square, 1, 2)
-        after(1, group_h, 1, 0)
         after(1, normalise, 1, 1)
         after(1, square, 1, 3)
-        after(1, group_h, 1, 1)
+        after(1, group_weight, Q, 1, 0, "scalar")
         after(1, group_weight, Q, 1, 1, "scalar")
+        after(1, group_h, 1, 0)
+        after(1, group_h, 1, 1)
         after(3, normalise, 1, 2)
         after(3, normalise, 1, 3)
-        after(3, quantise_h, 1, 0)
-        after(3, quantise_h, 1, 1)
         after(3, group_h, 1, 2)
         after(3, quantise_weight, Q, 1)
-        after(3, group_weight, K, 0, 0, "scalar")
         after(3, group_h, 1, 3)
+        after(3, group_weight, K, 0, 0, "scalar")
         after(3, group_weight, K, 0, 1, "scalar")
-        after(5, quantise_h, 1, 2)
-        after(5, quantise_h, 1, 3)
-        for i, (m, c, g) in enumerate(regroupings):
-            after(7 + 2 * (i // 2), group_weight, m, c, g, "scalar")
-        after(11, quantise_weight, K, 0)
-        after(13, quantise_weight, V, 0)
-        after(17, quantise_weight, K, 1)
-        after(19, quantise_weight, V, 1)
+        after(3, group_weight, V, 0, 0, "scalar")
+        after(3, group_weight, V, 0, 1, "scalar")
+        after(5, quantise_h, 1, 0, SUB)
+        after(9, quantise_weight, K, 0)
+        after(10, quantise_weight, V, 0)
+        after(11, group_weight, K, 1, 0, "scalar")
+        after(13, group_weight, K, 1, 1, "scalar")
+        after(15, group_weight, V, 1, 0, "scalar")
+        after(17, group_weight, V, 1, 1, "scalar")
+        after(18, quantise_weight, K, 1)
+        after(20, quantise_weight, V, 1)
         plain = [(b, s, c) for c in range(N_CHUNKS) for b in range(BATCH) for s in range(SUB)]
         for n, (b, s, c) in enumerate(plain):
-            i = 15 + n * 2 // 3
+            i = 11 + n if c == 0 else 20 + (n - 8) * 2 // 3
             after(i, plain_unit, b, s, c)
             if s == SUB - 1:
                 after(i, store, V, b, c)
@@ -429,33 +392,21 @@ def tile_flexattentionblock_pa_kernel(tc, x, attn_norm_w, wq, wk, wv, out_0, out
                 project(m, b, s, c, acc)
                 banks[i] = acc
                 started.append(i)
-                if m in SPLIT and s % 2 == 1:
-                    sums = psum_sum.tile([P, 2, N_TILE // 2], F32)
-                    for n in range(2):
-                        project_sum(b, s - 1 + n, c, sums[:, n, :])
-                    banks[i, "sum"] = sums
 
         start_rotations(2)
         for i, (m, b, s, c) in enumerate(rotations):
             if i < len(rotations) - SUB:
                 y = result(m, b, c)
             adder = nc.vector if i in VECTOR_SUMS else nc.gpsimd
-            if m not in SPLIT:
-                start_rotations(i + LOOKAHEAD + 1)
-                if i < len(rotations) - SUB:
-                    rotate(banks[i], s, y[:, :, s, :], adder)
-                else:
-                    y_last = last_pool.tile([P, N_HEADS, HEAD_DIM], F32)
-                    rotate(banks[i], s, y_last[:], adder)
-                    store_tile(m, b, s, c, y_last)
-            elif s % 2 == 1:
-                start_rotations(i + 3)
-                rotate_pair(
-                    [banks[i - 1], banks[i]], banks[i, "sum"], s - 1, [y[:, :, s - 1, :], y[:, :, s, :]],
-                    [nc.gpsimd, nc.gpsimd],
-                )
+            start_rotations(i + LOOKAHEAD + 1)
+            if i < len(rotations) - SUB:
+                rotate(banks[i], s, y[:, :, s, :], adder)
+            else:
+                y_last = last_pool.tile([P, N_HEADS, HEAD_DIM], F32)
+                rotate(banks[i], s, y_last[:], adder)
+                store_tile(m, b, s, c, y_last)
             if s == SUB - 1 and i < len(rotations) - SUB:
                 store(m, b, c)
             for f, args in side.get(i, []):
                 f(*args)
-                start_rotations(i + 3)
+                start_rotations(i + LOOKAHEAD + 1)

@@ -50,11 +50,11 @@ def tile_flexattentionblock_pa_kernel(tc, x, attn_norm_w, wq, wk, wv, out_0, out
     with ExitStack() as ctx:
         const = ctx.enter_context(tc.tile_pool(name="const", bufs=1))
         resident = ctx.enter_context(tc.tile_pool(name="resident", bufs=1))
-        squares_pool = ctx.enter_context(tc.tile_pool(name="squares", bufs=2))
+        squares_pool = ctx.enter_context(tc.tile_pool(name="squares", bufs=1))
         h_pool = ctx.enter_context(tc.tile_pool(name="h", bufs=4))
-        w_grouped_pool = ctx.enter_context(tc.tile_pool(name="w_grouped", bufs=4))
+        w_grouped_pool = ctx.enter_context(tc.tile_pool(name="w_grouped", bufs=2))
         rot_pool = ctx.enter_context(tc.tile_pool(name="rot", bufs=4))
-        y_pool = ctx.enter_context(tc.tile_pool(name="y", bufs=4))
+        y_pool = ctx.enter_context(tc.tile_pool(name="y", bufs=6))
         last_pool = ctx.enter_context(tc.tile_pool(name="last", bufs=SUB))
         psum_gain = ctx.enter_context(tc.psum_pool(name="psum_gain", bufs=1))
         psum_aux = ctx.enter_context(tc.psum_pool(name="psum_aux", bufs=2))
@@ -103,8 +103,6 @@ def tile_flexattentionblock_pa_kernel(tc, x, attn_norm_w, wq, wk, wv, out_0, out
         load_weight(K)
         load_weight(V)
 
-        ident_bf16 = const.tile([P, P], BF16)
-        make_identity(nc, ident_bf16[:])
         ident = const.tile([P, P], F32)
         make_identity(nc, ident[:])
         neg_half = const.tile([P, 1], F32)
@@ -226,30 +224,6 @@ def tile_flexattentionblock_pa_kernel(tc, x, attn_norm_w, wq, wk, wv, out_0, out
                 in_=src.rearrange("p t (a i) -> p a t i", i=4),
             )
 
-        moved = {}
-
-        def move_weight(c, g):
-            half = N_TILE // 2
-            for a in range(2):
-                bank = psum.tile([P, half, PACK], BF16, tag="acc")
-                for t in range(0, PACK, 2):
-                    nc.tensor.matmul(
-                        out=bank[:, :, t : t + 2],
-                        lhsT=ident_bf16[:],
-                        rhs=wq_raw[c][:, g, t : t + 2, a * half : (a + 1) * half].rearrange("p t n -> p n t"),
-                        start=True,
-                        stop=True,
-                    )
-                moved[c, g, a] = bank
-
-        def take_weight(c, g, copy):
-            half = N_TILE // 2
-            if (Q, c) not in w_words:
-                w_grouped = w_grouped_pool.tile([P, PASSES, N_TILE, PACK], BF16, align_bytes=64)
-                w_words[Q, c] = w_grouped
-            for a in range(2):
-                copy(out=w_words[Q, c][:, g, a * half : (a + 1) * half, :], in_=moved[c, g, a][:])
-
         def quantise_weight(m, c):
             nc.vector.quantize_mx(
                 out=w_codes[m][:, c, :, :].rearrange("p g n -> p (g n)").bitcast(FP8X4),
@@ -281,8 +255,8 @@ def tile_flexattentionblock_pa_kernel(tc, x, attn_norm_w, wq, wk, wv, out_0, out
             for product, factor, table in ((direct, u, cos_table), (crossed, u[:, :, :, ::-1], sin_table)):
                 nc.vector.tensor_tensor(
                     out=product[:],
-                    in0=factor,
-                    in1=table[:, s, :, :].unsqueeze(1).to_broadcast(rot_shape),
+                    in0=table[:, s, :, :].unsqueeze(1).to_broadcast(rot_shape),
+                    in1=factor,
                     op=ALU.mult,
                 )
             adder.tensor_tensor(
@@ -321,16 +295,13 @@ def tile_flexattentionblock_pa_kernel(tc, x, attn_norm_w, wq, wk, wv, out_0, out
         make_turns()
         for s in range(SUB):
             square(0, s)
-        move_weight(0, 0)
-        normalise(0, 0)
-        move_weight(0, 1)
-        for s in range(1, SUB):
-            normalise(0, s)
-            if s < 3:
-                group_h(0, s - 1)
-        take_weight(0, 0, nc.vector.tensor_copy)
-        take_weight(0, 1, nc.scalar.copy)
         make_tables()
+        for s in range(SUB):
+            normalise(0, s)
+            if s < 2:
+                group_h(0, s)
+        group_weight(Q, 0, 0, "vector")
+        group_weight(Q, 0, 1, "scalar")
         quantise_h(0, 0)
         quantise_h(0, 1)
         quantise_weight(Q, 0)
@@ -353,11 +324,11 @@ def tile_flexattentionblock_pa_kernel(tc, x, attn_norm_w, wq, wk, wv, out_0, out
         after(1, group_weight, Q, 1, 1, "scalar")
         after(1, group_h, 1, 0)
         after(1, group_h, 1, 1)
-        after(3, normalise, 1, 2)
-        after(3, normalise, 1, 3)
-        after(3, group_h, 1, 2)
-        after(3, quantise_weight, Q, 1)
-        after(3, group_h, 1, 3)
+        after(2, normalise, 1, 2)
+        after(2, normalise, 1, 3)
+        after(2, group_h, 1, 2)
+        after(2, quantise_weight, Q, 1)
+        after(2, group_h, 1, 3)
         after(3, group_weight, K, 0, 0, "scalar")
         after(3, group_weight, K, 0, 1, "scalar")
         after(3, group_weight, V, 0, 0, "scalar")

@@ -276,7 +276,8 @@ def tile_flexattentionblock_pa_kernel(tc, x, attn_norm_w, wq, wk, wv, out_0, out
 
         def store(m, b, c):
             heads = slice(c * N_HEADS, (c + 1) * N_HEADS)
-            nc.sync.dma_start(
+            queue = nc.scalar if m == V else nc.sync
+            queue.dma_start(
                 out=outs[m][b, heads, :, :].rearrange("h (p s) d -> p h (s d)", s=SUB),
                 in_=results[m, b, c][:].rearrange("p h s d -> p h (s d)"),
             )

import math
from contextlib import ExitStack

import concourse.mybir as mybir
from concourse.masks import make_identity

FP8X4 = mybir.dt.float8_e4m3fn_x4
BF16 = mybir.dt.bfloat16
F32 = mybir.dt.float32
I32 = mybir.dt.int32
U32 = mybir.dt.uint32
U8 = mybir.dt.uint8
ALU = mybir.AluOpType
ACT = mybir.ActivationFunctionType

P = 128
BATCH = 2
SEQ = 512
DIM = 1024
HEADS = 8
HEAD_DIM = 128
PAIRS = HEAD_DIM // 2
QD = HEADS * HEAD_DIM
THETA = 10000.0
EPS = 1e-6

PACK = 4
K_PASS = P * PACK
PASSES = DIM // K_PASS
SUB = SEQ // P
N_TILE = 512
N_HEADS = N_TILE // HEAD_DIM
N_CHUNKS = QD // N_TILE
K_PAIRS = PACK // 2

VECTOR_SUMS = (29, 31)
LOOKAHEAD = 3

ROUND_MAGIC = 12582912.0

FLOPS = 2 * BATCH * SEQ * DIM * 3 * QD


def tile_flexattentionblock_pa_kernel(tc, x, attn_norm_w, wq, wk, wv, out_0, out_1, out_2):
    nc = tc.nc
    weights = (wq, wk, wv)
    outs = (out_0, out_1, out_2)
    Q, K, V = 0, 1, 2

    with ExitStack() as ctx:
        const = ctx.enter_context(tc.tile_pool(name="const", bufs=1))
        resident = ctx.enter_context(tc.tile_pool(name="resident", bufs=1))
        squares_pool = ctx.enter_context(tc.tile_pool(name="squares", bufs=1))
        h_pool = ctx.enter_context(tc.tile_pool(name="h", bufs=4))
        w_grouped_pool = ctx.enter_context(tc.tile_pool(name="w_grouped", bufs=2))
        rot_pool = ctx.enter_context(tc.tile_pool(name="rot", bufs=4))
        y_pool = ctx.enter_context(tc.tile_pool(name="y", bufs=6))
        last_pool = ctx.enter_context(tc.tile_pool(name="last", bufs=SUB))
        psum_gain = ctx.enter_context(tc.psum_pool(name="psum_gain", bufs=1))
        psum_aux = ctx.enter_context(tc.psum_pool(name="psum_aux", bufs=2))
        psum = ctx.enter_context(tc.psum_pool(name="psum", bufs=5))
        ctx.enter_context(tc.manual_schedule())

        sin_probe = const.tile([P, 1], F32)
        nc.vector.memset(sin_probe[:], 0.0)
        nc.scalar.activation(out=sin_probe[:], in_=sin_probe[:], func=ACT.Sin)
        ones = const.tile([P, P], BF16)
        nc.vector.memset(ones[:], 1.0)
        pos_int = const.tile([P, SUB], I32)
        nc.gpsimd.iota(pos_int[:], pattern=[[1, SUB]], base=0, channel_multiplier=SUB)

        gain_row = const.tile([P, DIM], BF16)
        nc.gpsimd.memset(gain_row[:].bitcast(I32), 0)

        x_sb = [resident.tile([P, SUB, DIM], BF16, name="x_sb%d" % b) for b in range(BATCH)]
        wq_raw = [resident.tile([P, PASSES, PACK, N_TILE], BF16, name="wq_raw%d" % c) for c in range(N_CHUNKS)]
        w_raw = [
            [resident.tile([P, PACK, QD], BF16, name="w_raw%d_%d" % (m, g)) for g in range(PASSES)]
            for m in (K, V)
        ]
        by_pass = [w.rearrange("(g p t) n -> g p t n", t=PACK, p=P) for w in weights]

        def load_x(b, s):
            nc.sync.dma_start(out=x_sb[b][:, s, :], in_=x[b, :, :].rearrange("(p s) k -> p s k", s=SUB)[:, s, :])

        def load_wq(c):
            for g in range(PASSES):
                nc.sync.dma_start(
                    out=wq_raw[c][:, g, :, :], in_=by_pass[Q][g, :, :, c * N_TILE : (c + 1) * N_TILE]
                )

        def load_weight(m):
            for g in range(PASSES):
                nc.sync.dma_start(out=w_raw[m - K][g][:], in_=by_pass[m][g, :, :, :])

        load_x(0, 0)
        nc.sync.dma_start(out=gain_row[0:1, :], in_=attn_norm_w.rearrange("(o k) -> o k", o=1))
        for s in range(1, SUB):
            load_x(0, s)
        load_wq(0)
        nc.sync.dma_start(out=x_sb[1][:], in_=x[1, :, :].rearrange("(p s) k -> p s k", s=SUB))
        load_wq(1)
        load_weight(K)
        load_weight(V)

        ident = const.tile([P, P], F32)
        make_identity(nc, ident[:])
        neg_half = const.tile([P, 1], F32)
        nc.gpsimd.memset(neg_half[:], -0.5)

        gain = psum_gain.tile([P, DIM], BF16)
        for half in range(DIM // N_TILE):
            cols = slice(half * N_TILE, (half + 1) * N_TILE)
            nc.tensor.matmul(out=gain[:, cols], lhsT=ones[:], rhs=gain_row[:, cols], start=True, stop=True)

        table_shape = [P, SUB, PAIRS]
        pair_shape = [P, SUB, PAIRS, 2]
        turns = const.tile(table_shape, F32)
        whole = const.tile(table_shape, F32)
        sin_turns = const.tile(pair_shape, F32)
        size_turns = const.tile(table_shape, F32)
        cos_table = const.tile(pair_shape, F32)
        sin_table = const.tile(pair_shape, F32)

        def make_turns():
            nc.vector.tensor_scalar_mul(out=turns[:, :, 0], in0=pos_int[:], scalar1=1.0 / (2.0 * math.pi))
            width = 1
            while width < PAIRS:
                for n in range(1, 4):
                    nc.vector.tensor_scalar_mul(
                        out=turns[:, :, n * width : (n + 1) * width],
                        in0=turns[:, :, 0:width],
                        scalar1=THETA ** (-2.0 * n * width / HEAD_DIM),
                    )
                width *= 4
            nc.vector.tensor_scalar(
                out=whole[:], in0=turns[:], scalar1=ROUND_MAGIC, scalar2=ROUND_MAGIC, op0=ALU.add, op1=ALU.subtract
            )
            nc.vector.tensor_tensor(out=sin_turns[:, :, :, 1], in0=turns[:], in1=whole[:], op=ALU.subtract)
            nc.vector.tensor_tensor(out=sin_turns[:, :, :, 0], in0=whole[:], in1=turns[:], op=ALU.subtract)
            nc.vector.tensor_tensor(
                out=size_turns[:], in0=sin_turns[:, :, :, 0], in1=sin_turns[:, :, :, 1], op=ALU.max
            )

        def make_tables():
            nc.scalar.activation(out=sin_table[:], in_=sin_turns[:], func=ACT.Sin, scale=2.0 * math.pi)
            nc.scalar.activation(
                out=cos_table[:],
                in_=size_turns[:].unsqueeze(3).to_broadcast(pair_shape),
                func=ACT.Sin,
                scale=-2.0 * math.pi,
                bias=math.pi / 2.0,
            )

        h_codes = resident.tile([P, BATCH * SUB * PASSES * P], U32, align_bytes=64)
        h_scales = resident.tile([P, BATCH * SUB * PASSES * P], U8, align_bytes=64)
        mean_sq = const.tile([P, BATCH * SUB], F32)
        mean_eps = const.tile([P, BATCH * SUB], F32)
        rstd = const.tile([P, BATCH * SUB], F32)
        ready = set()
        h_planes = {}
        h_words = {}
        h_batch = const.tile([P, SUB * DIM], BF16, align_bytes=64)

        def square(b, s):
            one = slice(b * SUB + s, b * SUB + s + 1)
            squares = squares_pool.tile([P, DIM], BF16)
            nc.scalar.activation(
                out=squares[:], in_=x_sb[b][:, s, :], func=ACT.Square, scale=1.0 / math.sqrt(DIM), accum_out=mean_sq[:, one]
            )
            nc.gpsimd.tensor_scalar(out=mean_eps[:, one], in0=mean_sq[:, one], scalar1=EPS, scalar2=None, op0=ALU.add)
            nc.gpsimd.tensor_tensor(out=rstd[:, one], in0=mean_eps[:, one], in1=neg_half[:], op=ALU.pow)

        def normalise(b, s):
            one = slice(b * SUB + s, b * SUB + s + 1)
            h = h_pool.tile([P, DIM], BF16)
            nc.vector.scalar_tensor_tensor(
                out=h[:], in0=x_sb[b][:, s, :], scalar=rstd[:, one], in1=gain[:], op0=ALU.mult, op1=ALU.mult
            )
            words = h[:].bitcast(F32)
            h_t = psum_aux.tile([P, PASSES, K_PAIRS, P], F32, tag="aux")
            for g in range(PASSES):
                for u in range(K_PAIRS):
                    nc.tensor.transpose(
                        h_t[:, g, u, :], words[:, K_PAIRS * P * g + u : K_PAIRS * P * (g + 1) : K_PAIRS], ident[:]
                    )
            h_planes[b, s] = h_t

        def group_h(b, s):
            if b == 0:
                h_grouped = h_pool.tile([P, PASSES * P * PACK], BF16, align_bytes=64)
                h_words[b, s] = h_grouped[:]
            else:
                h_words[b, s] = h_batch[:, s * DIM : (s + 1) * DIM]
            nc.scalar.copy(
                out=h_words[b, s].bitcast(F32).rearrange("p (g r u) -> p g r u", g=PASSES, u=K_PAIRS),
                in_=h_planes[b, s][:].rearrange("p g u r -> p g r u"),
            )

        def quantise_h(b, s, tiles=1):
            i = b * SUB + s
            cols = slice(i * PASSES * P, (i + tiles) * PASSES * P)
            nc.vector.quantize_mx(
                out=h_codes[:, cols].bitcast(FP8X4),
                scales=h_scales[:, cols],
                in_=h_words[b, s] if tiles == 1 else h_batch[:, s * DIM : (s + tiles) * DIM],
            )
            for n in range(tiles):
                ready.add(("h", b, s + n))

        w_codes = [resident.tile([P, N_CHUNKS, PASSES, N_TILE], U32, name="w_codes%d" % m, align_bytes=64) for m in range(3)]
        w_scales = [resident.tile([P, N_CHUNKS, PASSES, N_TILE], U8, name="w_scales%d" % m, align_bytes=64) for m in range(3)]
        w_words = {}

        def group_weight(m, c, g, engine):
            if (m, c) not in w_words:
                w_grouped = w_grouped_pool.tile([P, PASSES, N_TILE, PACK], BF16, align_bytes=64)
                w_words[m, c] = w_grouped
            src = wq_raw[c][:, g, :, :] if m == Q else w_raw[m - K][g][:, :, c * N_TILE : (c + 1) * N_TILE]
            copy = nc.scalar.copy if engine == "scalar" else nc.vector.tensor_copy
            out = w_words[m, c][:, g, :, :]
            copy(
                out=out.rearrange("p (a i) t -> p a t i", i=4),
                in_=src.rearrange("p t (a i) -> p a t i", i=4),
            )

        def quantise_weight(m, c):
            nc.vector.quantize_mx(
                out=w_codes[m][:, c, :, :].rearrange("p g n -> p (g n)").bitcast(FP8X4),
                scales=w_scales[m][:, c, :, :].rearrange("p g n -> p (g n)"),
                in_=w_words[m, c][:].rearrange("p g n t -> p (g n t)"),
            )
            ready.add(("w", m, c))

        def project(m, b, s, c, acc):
            i = b * SUB + s
            for g in range(PASSES):
                tokens = slice((i * PASSES + g) * P, (i * PASSES + g + 1) * P)
                nc.tensor.matmul_mx(
                    out=acc[:],
                    lhsT=h_codes[:, tokens].bitcast(FP8X4),
                    lhsT_scale=h_scales[:, tokens],
                    rhs=w_codes[m][:, c, g, :].bitcast(FP8X4),
                    rhs_scale=w_scales[m][:, c, g, :],
                    start=(g == 0),
                    stop=(g == PASSES - 1),
                )

        rot_shape = [P, N_HEADS, PAIRS, 2]

        def rotate(acc, s, y, adder):
            u = acc[:].rearrange("p (h j r) -> p h j r", j=PAIRS, r=2)
            direct = rot_pool.tile(rot_shape, F32, tag="direct")
            crossed = rot_pool.tile(rot_shape, F32, tag="crossed")
            for product, factor, table in ((direct, u, cos_table), (crossed, u[:, :, :, ::-1], sin_table)):
                nc.vector.tensor_tensor(
                    out=product[:],
                    in0=table[:, s, :, :].unsqueeze(1).to_broadcast(rot_shape),
                    in1=factor,
                    op=ALU.mult,
                )
            adder.tensor_tensor(
                out=y,
                in0=direct[:].rearrange("p h j r -> p h (j r)"),
                in1=crossed[:].rearrange("p h j r -> p h (j r)"),
                op=ALU.add,
            )

        results = {}

        def result(m, b, c):
            if (m, b, c) not in results:
                y_tile = y_pool.tile([P, N_HEADS, SUB, HEAD_DIM], F32)
                results[m, b, c] = y_tile
            return results[m, b, c]

        def store(m, b, c):
            heads = slice(c * N_HEADS, (c + 1) * N_HEADS)
            queue = nc.scalar if m == V else nc.sync
            queue.dma_start(
                out=outs[m][b, heads, :, :].rearrange("h (p s) d -> p h (s d)", s=SUB),
                in_=results[m, b, c][:].rearrange("p h s d -> p h (s d)"),
            )

        def store_tile(m, b, s, c, y_tile):
            heads = slice(c * N_HEADS, (c + 1) * N_HEADS)
            nc.sync.dma_start(
                out=outs[m][b, heads, :, :].rearrange("h (p s) d -> p h s d", s=SUB)[:, :, s, :], in_=y_tile[:]
            )

        def plain_unit(b, s, c):
            acc = psum_aux.tile([P, N_TILE], F32, tag="aux")
            project(V, b, s, c, acc)
            nc.scalar.copy(out=result(V, b, c)[:, :, s, :], in_=acc[:].rearrange("p (h d) -> p h d", d=HEAD_DIM))

        make_turns()
        for s in range(SUB):
            square(0, s)
        make_tables()
        for s in range(SUB):
            normalise(0, s)
            if s < 2:
                group_h(0, s)
        group_weight(Q, 0, 0, "vector")
        group_weight(Q, 0, 1, "scalar")
        quantise_h(0, 0)
        quantise_h(0, 1)
        quantise_weight(Q, 0)
        for s in (2, 3):
            group_h(0, s)
            quantise_h(0, s)
        square(1, 0)
        square(1, 1)

        side = {}

        def after(i, f, *args):
            side.setdefault(i, []).append((f, args))

        after(1, normalise, 1, 0)
        after(1, square, 1, 2)
        after(1, normalise, 1, 1)
        after(1, square, 1, 3)
        after(1, group_weight, Q, 1, 0, "scalar")
        after(1, group_weight, Q, 1, 1, "scalar")
        after(1, group_h, 1, 0)
        after(1, group_h, 1, 1)
        after(2, normalise, 1, 2)
        after(2, normalise, 1, 3)
        after(2, group_h, 1, 2)
        after(2, quantise_weight, Q, 1)
        after(2, group_h, 1, 3)
        after(3, group_weight, K, 0, 0, "scalar")
        after(3, group_weight, K, 0, 1, "scalar")
        after(3, group_weight, V, 0, 0, "scalar")
        after(3, group_weight, V, 0, 1, "scalar")
        after(5, quantise_h, 1, 0, SUB)
        after(9, quantise_weight, K, 0)
        after(10, quantise_weight, V, 0)
        after(11, group_weight, K, 1, 0, "scalar")
        after(13, group_weight, K, 1, 1, "scalar")
        after(15, group_weight, V, 1, 0, "scalar")
        after(17, group_weight, V, 1, 1, "scalar")
        after(18, quantise_weight, K, 1)
        after(20, quantise_weight, V, 1)
        plain = [(b, s, c) for c in range(N_CHUNKS) for b in range(BATCH) for s in range(SUB)]
        for n, (b, s, c) in enumerate(plain):
            i = 11 + n if c == 0 else 20 + (n - 8) * 2 // 3
            after(i, plain_unit, b, s, c)
            if s == SUB - 1:
                after(i, store, V, b, c)

        groups = [(Q, 0, 0), (Q, 0, 1), (Q, 1, 0), (Q, 1, 1), (K, 0, 0), (K, 1, 0), (K, 0, 1), (K, 1, 1)]
        rotations = [(m, b, s, c) for m, b, c in groups for s in range(SUB)]
        banks = {}
        started = []

        def start_rotations(end):
            for i in range(len(started), min(end, len(rotations))):
                m, b, s, c = rotations[i]
                if ("h", b, s) not in ready or ("w", m, c) not in ready:
                    break
                acc = psum.tile([P, N_TILE], F32, tag="acc")
                project(m, b, s, c, acc)
                banks[i] = acc
                started.append(i)

        start_rotations(2)
        for i, (m, b, s, c) in enumerate(rotations):
            if i < len(rotations) - SUB:
                y = result(m, b, c)
            adder = nc.vector if i in VECTOR_SUMS else nc.gpsimd
            start_rotations(i + LOOKAHEAD + 1)
            if i < len(rotations) - SUB:
                rotate(banks[i], s, y[:, :, s, :], adder)
            else:
                y_last = last_pool.tile([P, N_HEADS, HEAD_DIM], F32)
                rotate(banks[i], s, y_last[:], adder)
                store_tile(m, b, s, c, y_last)
            if s == SUB - 1 and i < len(rotations) - SUB:
                store(m, b, c)
            for f, args in side.get(i, []):
                f(*args)
                start_rotations(i + LOOKAHEAD + 1)
